import numpy as np
import ml_dtypes


def mxq(x, axis, fmt="e4m3"):
    dtype, down = {"e4m3": (ml_dtypes.float8_e4m3fn, 7), "e5m2": (ml_dtypes.float8_e5m2, 14)}[fmt]
    v = np.moveaxis(np.asarray(x, np.float32).astype(ml_dtypes.bfloat16).astype(np.float64), axis, -1)
    blocks = v.reshape(v.shape[:-1] + (-1, 32))
    amax = np.abs(blocks).max(-1, keepdims=True)
    byte = np.maximum(np.where(amax > 0, np.frexp(amax)[1] - 1 + 127, 0) - down, 1)
    scale = np.exp2(byte - 127.0)
    codes = (blocks / scale).astype(np.float32).astype(dtype).astype(np.float64)
    return np.moveaxis((codes * scale).reshape(v.shape), -1, axis)


WIDE = False


def mx_kscale(k):
    if not WIDE:
        return np.ones(k)
    levels = np.array([10, -10, 5, -5, 0])
    a = np.random.permutation(np.resize(levels, k // 512 * 4)).reshape(k // 512, 4)
    idx = np.arange(k)
    return np.exp2(a[idx // 512, idx % 128 // 32])


BF16 = ml_dtypes.bfloat16


def bf(x):
    return np.asarray(x, np.float32).astype(BF16)


def f64(x):
    return np.asarray(x).astype(np.float64)


E2M1 = np.array([0.0, 0.5, 1.0, 1.5, 2.0, 3.0, 4.0, 6.0, -0.0, -0.5, -1.0, -1.5, -2.0, -3.0, -4.0, -6.0])


def pack_weight(w, fmt):
    k, n = w.shape
    w = f64(bf(w)).reshape(k // 32, 32, n)
    amax = np.abs(w).max(1)
    if fmt == "e4m3":
        byte = np.frexp(amax)[1] - 1 + 127 - 7
    else:
        mant, ex = np.frexp(amax / 6.0)
        byte = np.where(mant > 0.5, ex, ex - 1) + 127
    byte = np.clip(np.where(amax > 0, byte, 1), 1, 254)
    scaled = (w * np.exp2(127.0 - byte)[:, None, :]).reshape(k, n).astype(np.float32)
    by_word = np.ascontiguousarray(scaled.reshape(k // 512, 128, 4, n).transpose(0, 1, 3, 2))
    if fmt == "e4m3":
        words = by_word.astype(ml_dtypes.float8_e4m3fn).view(np.uint8)
    else:
        c = by_word.astype(ml_dtypes.float4_e2m1fn).view(np.uint8) & 0xF
        words = c[..., 0::2] | (c[..., 1::2] << 4)
    return np.ascontiguousarray(words), np.ascontiguousarray(byte.astype(np.uint8).reshape(k // 512, 16, n))


def unpack_weight(words, scales, fmt):
    g, p, n, _ = words.shape
    if fmt == "e4m3":
        vals = np.ascontiguousarray(words).view(ml_dtypes.float8_e4m3fn).astype(np.float64)
    else:
        nib = np.empty((g, p, n, 4), np.uint8)
        nib[..., 0::2] = words & 0xF
        nib[..., 1::2] = words >> 4
        vals = E2M1[nib]
    vals = vals * np.repeat(np.exp2(scales.astype(np.float64) - 127.0), 8, axis=1)[..., None]
    return vals.transpose(0, 1, 3, 2).reshape(g * 512, n)


B, I, H, C, S = 4096, 384, 128, 1023, 3
EPSILON = 1e-6
CC = 1 + C
K = I + H
FMT = "e4m3"


def setup_inputs():
    s = mx_kscale(K)
    t = mx_kscale(CC)
    t = t / t.min()
    invariant_input = bf(np.random.standard_normal((B, I)) * s[:I])
    equivariant_input = bf(np.random.standard_normal((B, S)) * 0.125 * t[0])
    invariant_hidden = bf(np.random.standard_normal((B, H)) * s[I:])
    equivariant_hidden = bf(np.random.standard_normal((B, S, C)) * 0.125 * t[1:])
    W_left_words, W_left_scales = pack_weight(np.random.standard_normal((CC, H)) * 0.15 / np.sqrt(CC) * t[:, None], FMT)
    W_right_words, W_right_scales = pack_weight(np.random.standard_normal((CC, H)) * 0.15 / np.sqrt(CC) * t[:, None], FMT)
    W_ii_words, W_ii_scales = pack_weight(np.random.standard_normal((K, H)) * 0.6 / np.sqrt(K) / s[:, None], FMT)
    b_ii = bf(np.random.standard_normal(H) * 0.3)
    return {
        "invariant_input": invariant_input,
        "equivariant_input": equivariant_input,
        "invariant_hidden": invariant_hidden,
        "equivariant_hidden": equivariant_hidden,
        "W_left_words": W_left_words,
        "W_left_scales": W_left_scales,
        "W_right_words": W_right_words,
        "W_right_scales": W_right_scales,
        "W_ii_words": W_ii_words,
        "W_ii_scales": W_ii_scales,
        "b_ii": b_ii,
    }


def reference(invariant_input, equivariant_input, invariant_hidden, equivariant_hidden, W_left_words, W_left_scales, W_right_words, W_right_scales, W_ii_words, W_ii_scales, b_ii):
    eq_comb = np.concatenate([f64(equivariant_input)[..., None], f64(equivariant_hidden)], axis=-1)
    inv_comb = np.concatenate([f64(invariant_input), f64(invariant_hidden)], axis=-1)
    norm = np.sum(eq_comb * eq_comb, axis=-2, keepdims=True) + EPSILON
    xn = mxq(eq_comb / norm, 2, "e4m3")
    left = xn @ unpack_weight(W_left_words, W_left_scales, FMT)
    right = xn @ unpack_weight(W_right_words, W_right_scales, FMT)
    proj = np.sum(left * right, axis=-2)
    lin = mxq(inv_comb, 1, "e4m3") @ unpack_weight(W_ii_words, W_ii_scales, FMT)
    return np.tanh(proj + lin + f64(b_ii))

@@ -1,0 +1,283 @@
+from contextlib import ExitStack
+
+import concourse.mybir as mybir
+from concourse.masks import make_identity
+
+F32 = mybir.dt.float32
+BF16 = mybir.dt.bfloat16
+I32 = mybir.dt.int32
+U32 = mybir.dt.uint32
+U8 = mybir.dt.uint8
+FP8X4 = mybir.dt.float8_e4m3fn_x4
+ACT = mybir.ActivationFunctionType
+ALU = mybir.AluOpType
+
+P = 128
+BATCH = 4096
+COMPONENTS = 3
+CHANNELS = 1024
+INPUT_FEATURES = 384
+FEATURES = 512
+HIDDEN = 128
+EPSILON = 1e-6
+PACK = 4
+K_PASS = P * PACK
+PASSES = CHANNELS // K_PASS
+TILES = BATCH // P
+INV_CHUNK = 8
+INV_LEAD = 4
+LOAD_AHEAD = 2
+FIRST_STORE_TILES = 24
+
+LEFT, RIGHT, LINEAR = 0, 2, 4
+WEIGHT_SLOTS = 5
+
+FLOPS = 2 * BATCH * HIDDEN * (2 * COMPONENTS * CHANNELS + FEATURES)
+
+
+def load_weight(nc, w_codes, w_planes, slot, words, scales):
+    passes = words.shape[0]
+    nc.sync.dma_start(
+        out=w_codes[:, slot : slot + passes, :].bitcast(I32),
+        in_=words.rearrange("g p n t -> p g (n t)").bitcast(I32),
+    )
+    for quadrant in range(4):
+        nc.sync.dma_start(
+            out=w_planes[32 * quadrant : 32 * quadrant + 4, slot : slot + passes, :].bitcast(I32),
+            in_=scales[:, 4 * quadrant : 4 * quadrant + 4, :].rearrange("g r n -> r g n").bitcast(I32),
+        )
+
+
+def tile_ryeelman_pa_t_kernel(
+    tc,
+    invariant_input,
+    equivariant_input,
+    invariant_hidden,
+    equivariant_hidden,
+    W_left_words,
+    W_left_scales,
+    W_right_words,
+    W_right_scales,
+    W_ii_words,
+    W_ii_scales,
+    b_ii,
+    out,
+):
+    nc = tc.nc
+    hidden_rows = equivariant_hidden.rearrange("(p t) j c -> t p j c", t=TILES)
+    inv_input_rows = invariant_input.rearrange("(p t) k -> p t k", t=TILES)
+    inv_hidden_rows = invariant_hidden.rearrange("(p t) k -> p t k", t=TILES)
+    out_rows = out.rearrange("(p t) h -> p t h", t=TILES)
+
+    with ExitStack() as ctx:
+        keep = ctx.enter_context(tc.tile_pool(name="keep", bufs=1))
+        inv_pool = ctx.enter_context(tc.tile_pool(name="inv", bufs=2))
+        x_pool = ctx.enter_context(tc.tile_pool(name="x", bufs=6))
+        work = ctx.enter_context(tc.tile_pool(name="work", bufs=2))
+        words_psum = ctx.enter_context(tc.psum_pool(name="words", bufs=4))
+        lengths_psum = ctx.enter_context(tc.psum_pool(name="lengths", bufs=2))
+        acc_psum = ctx.enter_context(tc.psum_pool(name="acc", bufs=1))
+        ctx.enter_context(tc.manual_schedule())
+
+        first_channel = keep.tile([P, TILES, COMPONENTS], BF16)
+        nc.sync.dma_start(out=first_channel[:], in_=equivariant_input.rearrange("(p t) j -> p t j", t=TILES))
+        w_codes = keep.tile([P, WEIGHT_SLOTS, PACK * HIDDEN], U8, align_bytes=64)
+        w_planes = keep.tile([P, WEIGHT_SLOTS, HIDDEN], U8, align_bytes=64)
+        nc.vector.memset(w_planes[:].bitcast(I32), 0)
+        zero = keep.tile([P, 1], F32)
+        nc.vector.memset(zero[:], 0.0)
+        epsilon = keep.tile([P, 1], F32)
+        nc.vector.tensor_scalar_add(out=epsilon[:], in0=zero[:], scalar1=EPSILON)
+        table_warmer = keep.tile([P, 1], F32)
+        nc.scalar.activation(out=table_warmer[:], in_=epsilon[:], func=ACT.Abs_reciprocal_sqrt)
+        identity = keep.tile([P, P], F32)
+        make_identity(nc, identity[:])
+        bias_rows = keep.tile([P, HIDDEN], BF16)
+
+        inv_codes = keep.tile([P, TILES, P], U32, align_bytes=64)
+        inv_planes = keep.tile([P, TILES, P], U8, align_bytes=64)
+        z_all = keep.tile([P, TILES, HIDDEN], F32)
+
+        inv_tiles = {}
+        x_tiles = {}
+        length2_tiles = {}
+        factor_tiles = {}
+        operand_tiles = {}
+
+        def load_invariants(chunk):
+            first = chunk * INV_CHUNK
+            inv_sb = inv_pool.tile([P, INV_CHUNK, FEATURES], BF16)
+            nc.sync.dma_start(out=inv_sb[:, :, 0:INPUT_FEATURES], in_=inv_input_rows[:, first : first + INV_CHUNK, :])
+            nc.sync.dma_start(
+                out=inv_sb[:, :, INPUT_FEATURES:FEATURES], in_=inv_hidden_rows[:, first : first + INV_CHUNK, :]
+            )
+            inv_tiles[chunk] = inv_sb
+
+        def quantise_invariants(chunk):
+            first = chunk * INV_CHUNK
+            inv_sb = inv_tiles[chunk]
+            inv_grouped = inv_pool.tile([P, INV_CHUNK * P, PACK], BF16, align_bytes=64)
+            for pair in range(INV_CHUNK // 2):
+                invT = words_psum.tile([P, 2, 2 * P], F32, tag="xT")
+                for i in range(2):
+                    inv_words = inv_sb[:, 2 * pair + i, :].bitcast(F32)
+                    for u in range(2):
+                        nc.tensor.transpose(
+                            invT[:, u, i * P : (i + 1) * P], inv_words[:, u : FEATURES // 2 : 2], identity[:]
+                        )
+                grouped_words = inv_grouped[:, 2 * pair * P : 2 * (pair + 1) * P, :].bitcast(F32)
+                if pair % 2 == 0:
+                    nc.scalar.copy(out=grouped_words, in_=invT[:].rearrange("p u c -> p c u"))
+                else:
+                    nc.vector.tensor_copy(out=grouped_words, in_=invT[:].rearrange("p u c -> p c u"))
+            nc.vector.quantize_mx(
+                out=inv_codes[:, first : first + INV_CHUNK, :].rearrange("p i b -> p (i b)").bitcast(FP8X4),
+                scales=inv_planes[:, first : first + INV_CHUNK, :].rearrange("p i b -> p (i b)"),
+                in_=inv_grouped[:].rearrange("p c t -> p (c t)"),
+            )
+
+        def linear(chunk):
+            for half, tag in enumerate(("left", "right")):
+                first = chunk * INV_CHUNK + half * (INV_CHUNK // 2)
+                lin_ps = acc_psum.tile([P, INV_CHUNK // 2, HIDDEN], F32, tag=tag)
+                for i in range(INV_CHUNK // 2):
+                    nc.tensor.matmul_mx(
+                        out=lin_ps[:, i, :],
+                        lhsT=inv_codes[:, first + i, :].bitcast(FP8X4),
+                        lhsT_scale=inv_planes[:, first + i, :],
+                        rhs=w_codes[:, LINEAR, :].bitcast(FP8X4),
+                        rhs_scale=w_planes[:, LINEAR, :],
+                        start=True,
+                        stop=True,
+                    )
+                nc.vector.tensor_tensor(
+                    out=z_all[:, first : first + INV_CHUNK // 2, :],
+                    in0=lin_ps[:],
+                    in1=bias_rows[:].unsqueeze(1).to_broadcast([P, INV_CHUNK // 2, HIDDEN]),
+                    op=ALU.add,
+                )
+
+        def load(t):
+            x_sb = x_pool.tile([P, COMPONENTS, CHANNELS], BF16)
+            nc.vector.tensor_copy(
+                out=x_sb[:, :, 0:2],
+                in_=first_channel[:, t, :].unsqueeze(2).to_broadcast([P, COMPONENTS, 2]),
+            )
+            nc.sync.dma_start(out=x_sb[:, :, 1:CHANNELS], in_=hidden_rows[t])
+            x_tiles[t] = x_sb
+
+        def squared_lengths(t):
+            x_sb = x_tiles[t]
+            squares = work.tile([P, COMPONENTS, CHANNELS], F32)
+            nc.scalar.activation(out=squares[:, 0:2, :], in_=x_sb[:, 0:2, :], func=ACT.Square)
+            nc.scalar.activation(out=squares[:, 2, :], in_=x_sb[:, 2, :], func=ACT.Square)
+            two_squares = work.tile([P, CHANNELS], F32)
+            nc.gpsimd.tensor_tensor(out=two_squares[:], in0=squares[:, 0, :], in1=squares[:, 1, :], op=ALU.add)
+            length2 = work.tile([P, CHANNELS], F32)
+            nc.gpsimd.tensor_tensor(out=length2[:], in0=two_squares[:], in1=squares[:, 2, :], op=ALU.add)
+            length2_tiles[t] = length2
+
+        def inverse_lengths(t):
+            length2 = length2_tiles[t]
+            inv_length = work.tile([P, PASSES, P, PACK], F32)
+            for g in range(PASSES):
+                length2T = lengths_psum.tile([P, PACK, P], F32)
+                for k in range(PACK):
+                    nc.tensor.transpose(
+                        length2T[:, k, :], length2[:, g * K_PASS + k : (g + 1) * K_PASS : PACK], identity[:]
+                    )
+                nc.scalar.activation(
+                    out=inv_length[:, g],
+                    in_=length2T[:].rearrange("p k b -> p b k"),
+                    func=ACT.Abs_reciprocal_sqrt,
+                    bias=epsilon[:],
+                    scale=1.0,
+                )
+            factor = work.tile([P, PASSES, P, PACK], F32)
+            nc.scalar.activation(out=factor[:], in_=inv_length[:], func=ACT.Square)
+            factor_tiles[t] = factor
+
+        def normalise_and_quantise(t):
+            x_sb = x_tiles[t]
+            factor = factor_tiles[t]
+            xn = work.tile([P, COMPONENTS, CHANNELS], BF16, align_bytes=64)
+            xn_codes = work.tile([P, COMPONENTS, PASSES * P], U32, align_bytes=64)
+            xn_planes = work.tile([P, COMPONENTS, PASSES * P], U8, align_bytes=64)
+            for j in range(COMPONENTS):
+                xT = words_psum.tile([P, 2, PASSES * P], F32, tag="xT")
+                x_words = x_sb[:, j, :].bitcast(F32)
+                for g in range(PASSES):
+                    for u in range(2):
+                        nc.tensor.transpose(
+                            xT[:, u, g * P : (g + 1) * P],
+                            x_words[:, g * 2 * P + u : (g + 1) * 2 * P : 2],
+                            identity[:],
+                        )
+                nc.vector.tensor_tensor(
+                    out=xn[:, j, :].rearrange("p (c u e) -> p c u e", u=2, e=2),
+                    in0=xT[:].bitcast(BF16).rearrange("p u (c e) -> p c u e", e=2),
+                    in1=factor[:].rearrange("p g b (u e) -> p (g b) u e", e=2),
+                    op=ALU.mult,
+                )
+            for j in range(COMPONENTS):
+                nc.vector.quantize_mx(out=xn_codes[:, j, :].bitcast(FP8X4), scales=xn_planes[:, j, :], in_=xn[:, j, :])
+            operand_tiles[t] = (xn_codes, xn_planes)
+
+        def project(t):
+            xn_codes, xn_planes = operand_tiles[t]
+            left_ps = acc_psum.tile([P, COMPONENTS, HIDDEN], F32, tag="left")
+            right_ps = acc_psum.tile([P, COMPONENTS, HIDDEN], F32, tag="right")
+            for side, acc in ((RIGHT, right_ps), (LEFT, left_ps)):
+                for j in range(COMPONENTS):
+                    for g in range(PASSES):
+                        nc.tensor.matmul_mx(
+                            out=acc[:, j, :],
+                            lhsT=xn_codes[:, j, g * P : (g + 1) * P].bitcast(FP8X4),
+                            lhsT_scale=xn_planes[:, j, g * P : (g + 1) * P],
+                            rhs=w_codes[:, side + g, :].bitcast(FP8X4),
+                            rhs_scale=w_planes[:, side + g, :],
+                            start=(g == 0),
+                            stop=(g == PASSES - 1),
+                        )
+            right_sb = work.tile([P, COMPONENTS, HIDDEN], F32)
+            nc.vector.tensor_copy(out=right_sb[:], in_=right_ps[:])
+            products = work.tile([P, COMPONENTS, HIDDEN], F32)
+            nc.vector.tensor_tensor(out=products[:], in0=left_ps[:], in1=right_sb[:], op=ALU.mult)
+            proj = work.tile([P, HIDDEN], F32)
+            nc.vector.tensor_reduce(
+                out=proj[:], in_=products[:].rearrange("p j h -> p h j"), axis=mybir.AxisListType.X, op=ALU.add
+            )
+            nc.vector.tensor_tensor(out=z_all[:, t, :], in0=proj[:], in1=z_all[:, t, :], op=ALU.add)
+
+        def finish(begin, end):
+            nc.scalar.activation(out=z_all[:, begin:end, :], in_=z_all[:, begin:end, :], func=ACT.Tanh)
+            nc.sync.dma_start(out=out_rows[:, begin:end, :], in_=z_all[:, begin:end, :])
+
+        load_weight(nc, w_codes, w_planes, LINEAR, W_ii_words, W_ii_scales)
+        load_invariants(0)
+        for t in range(LOAD_AHEAD):
+            load(t)
+        nc.sync.dma_start(out=bias_rows[:], in_=b_ii.partition_broadcast(P))
+        load_weight(nc, w_codes, w_planes, LEFT, W_left_words, W_left_scales)
+        load_weight(nc, w_codes, w_planes, RIGHT, W_right_words, W_right_scales)
+
+        for step in range(TILES + 3):
+            if step + LOAD_AHEAD < TILES:
+                load(step + LOAD_AHEAD)
+            if (step + INV_LEAD) % INV_CHUNK == 0 and step + INV_LEAD < TILES:
+                load_invariants((step + INV_LEAD) // INV_CHUNK)
+            if step % INV_CHUNK == 0 and step < TILES:
+                quantise_invariants(step // INV_CHUNK)
+            if step % INV_CHUNK == 1 and step < TILES:
+                linear(step // INV_CHUNK)
+            if 0 <= step - 2 < TILES:
+                normalise_and_quantise(step - 2)
+            if 0 <= step - 3 < TILES:
+                project(step - 3)
+            if step < TILES:
+                squared_lengths(step)
+            if 0 <= step - 1 < TILES:
+                inverse_lengths(step - 1)
+            if step - 3 == FIRST_STORE_TILES:
+                finish(0, FIRST_STORE_TILES)
+        finish(FIRST_STORE_TILES, TILES)

@@ -25,8 +25,9 @@ K_PASS = P * PACK
 PASSES = CHANNELS // K_PASS
 TILES = BATCH // P
 INV_CHUNK = 8
-INV_LEAD = 4
-LOAD_AHEAD = 2
+INV_CHUNKS = TILES // INV_CHUNK
+INV_PERIOD = 2
+LOAD_AHEAD = 3
 FIRST_STORE_TILES = 24
 
 LEFT, RIGHT, LINEAR = 0, 2, 4
@@ -72,7 +73,7 @@ def tile_ryeelman_pa_t_kernel(
     with ExitStack() as ctx:
         keep = ctx.enter_context(tc.tile_pool(name="keep", bufs=1))
         inv_pool = ctx.enter_context(tc.tile_pool(name="inv", bufs=2))
-        x_pool = ctx.enter_context(tc.tile_pool(name="x", bufs=6))
+        x_pool = ctx.enter_context(tc.tile_pool(name="x", bufs=LOAD_AHEAD + 4))
         work = ctx.enter_context(tc.tile_pool(name="work", bufs=2))
         words_psum = ctx.enter_context(tc.psum_pool(name="words", bufs=4))
         lengths_psum = ctx.enter_context(tc.psum_pool(name="lengths", bufs=2))
@@ -173,7 +174,7 @@ def tile_ryeelman_pa_t_kernel(
             nc.scalar.activation(out=squares[:, 2, :], in_=x_sb[:, 2, :], func=ACT.Square)
             two_squares = work.tile([P, CHANNELS], F32)
             nc.gpsimd.tensor_tensor(out=two_squares[:], in0=squares[:, 0, :], in1=squares[:, 1, :], op=ALU.add)
-            length2 = work.tile([P, CHANNELS], F32)
+            length2 = work.tile([P, CHANNELS], F32, bufs=3)
             nc.gpsimd.tensor_tensor(out=length2[:], in0=two_squares[:], in1=squares[:, 2, :], op=ALU.add)
             length2_tiles[t] = length2
 
@@ -253,31 +254,33 @@ def tile_ryeelman_pa_t_kernel(
             nc.scalar.activation(out=z_all[:, begin:end, :], in_=z_all[:, begin:end, :], func=ACT.Tanh)
             nc.sync.dma_start(out=out_rows[:, begin:end, :], in_=z_all[:, begin:end, :])
 
+        for t in range(LOAD_AHEAD - 1):
+            load(t)
         load_weight(nc, w_codes, w_planes, LINEAR, W_ii_words, W_ii_scales)
         load_invariants(0)
-        for t in range(LOAD_AHEAD):
-            load(t)
+        load(LOAD_AHEAD - 1)
         nc.sync.dma_start(out=bias_rows[:], in_=b_ii.partition_broadcast(P))
-        load_weight(nc, w_codes, w_planes, LEFT, W_left_words, W_left_scales)
-        load_weight(nc, w_codes, w_planes, RIGHT, W_right_words, W_right_scales)
 
-        for step in range(TILES + 3):
+        for step in range(TILES + 4):
             if step + LOAD_AHEAD < TILES:
                 load(step + LOAD_AHEAD)
-            if (step + INV_LEAD) % INV_CHUNK == 0 and step + INV_LEAD < TILES:
-                load_invariants((step + INV_LEAD) // INV_CHUNK)
-            if step % INV_CHUNK == 0 and step < TILES:
-                quantise_invariants(step // INV_CHUNK)
-            if step % INV_CHUNK == 1 and step < TILES:
-                linear(step // INV_CHUNK)
-            if 0 <= step - 2 < TILES:
-                normalise_and_quantise(step - 2)
+            if step % INV_PERIOD == 0 and step // INV_PERIOD + 1 < INV_CHUNKS:
+                load_invariants(step // INV_PERIOD + 1)
+            if step == 1:
+                load_weight(nc, w_codes, w_planes, LEFT, W_left_words, W_left_scales)
+                load_weight(nc, w_codes, w_planes, RIGHT, W_right_words, W_right_scales)
+            if step % INV_PERIOD == 0 and step // INV_PERIOD < INV_CHUNKS:
+                quantise_invariants(step // INV_PERIOD)
+            if step % INV_PERIOD == 1 and step // INV_PERIOD < INV_CHUNKS:
+                linear(step // INV_PERIOD)
             if 0 <= step - 3 < TILES:
-                project(step - 3)
+                normalise_and_quantise(step - 3)
+            if 0 <= step - 4 < TILES:
+                project(step - 4)
             if step < TILES:
                 squared_lengths(step)
-            if 0 <= step - 1 < TILES:
-                inverse_lengths(step - 1)
-            if step - 3 == FIRST_STORE_TILES:
+            if 0 <= step - 2 < TILES:
+                inverse_lengths(step - 2)
+            if step - 4 == FIRST_STORE_TILES:
                 finish(0, FIRST_STORE_TILES)
         finish(FIRST_STORE_TILES, TILES)

@@ -26,7 +26,6 @@ PASSES = CHANNELS // K_PASS
 TILES = BATCH // P
 INV_CHUNK = 8
 INV_CHUNKS = TILES // INV_CHUNK
-INV_PERIOD = 2
 LOAD_AHEAD = 3
 FIRST_STORE_TILES = 24
 
@@ -94,16 +93,27 @@ def tile_ryeelman_pa_t_kernel(
         identity = keep.tile([P, P], F32)
         make_identity(nc, identity[:])
         bias_rows = keep.tile([P, HIDDEN], BF16)
+        nc.sync.dma_start(out=bias_rows[:], in_=b_ii.partition_broadcast(P))
 
         inv_codes = keep.tile([P, TILES, P], U32, align_bytes=64)
         inv_planes = keep.tile([P, TILES, P], U8, align_bytes=64)
         z_all = keep.tile([P, TILES, HIDDEN], F32)
+        right_sets = []
+        term_sets = []
+        for parity in range(2):
+            right_and_one = keep.tile([P, COMPONENTS + 1, HIDDEN], F32, name="right_and_one%d" % parity)
+            nc.vector.memset(right_and_one[:, COMPONENTS, :], 1.0)
+            right_sets.append(right_and_one)
+            terms = keep.tile([P, COMPONENTS + 2, HIDDEN], F32, name="terms%d" % parity)
+            nc.vector.tensor_copy(out=terms[:, COMPONENTS + 1, :], in_=bias_rows[:])
+            term_sets.append(terms)
 
         inv_tiles = {}
         x_tiles = {}
         length2_tiles = {}
         factor_tiles = {}
         operand_tiles = {}
+        product_tiles = {}
 
         def load_invariants(chunk):
             first = chunk * INV_CHUNK
@@ -127,40 +137,16 @@ def tile_ryeelman_pa_t_kernel(
                             invT[:, u, i * P : (i + 1) * P], inv_words[:, u : FEATURES // 2 : 2], identity[:]
                         )
                 grouped_words = inv_grouped[:, 2 * pair * P : 2 * (pair + 1) * P, :].bitcast(F32)
-                if pair % 2 == 0:
-                    nc.scalar.copy(out=grouped_words, in_=invT[:].rearrange("p u c -> p c u"))
-                else:
-                    nc.vector.tensor_copy(out=grouped_words, in_=invT[:].rearrange("p u c -> p c u"))
+                nc.vector.tensor_copy(out=grouped_words, in_=invT[:].rearrange("p u c -> p c u"))
             nc.vector.quantize_mx(
                 out=inv_codes[:, first : first + INV_CHUNK, :].rearrange("p i b -> p (i b)").bitcast(FP8X4),
                 scales=inv_planes[:, first : first + INV_CHUNK, :].rearrange("p i b -> p (i b)"),
                 in_=inv_grouped[:].rearrange("p c t -> p (c t)"),
             )
 
-        def linear(chunk):
-            for half, tag in enumerate(("left", "right")):
-                first = chunk * INV_CHUNK + half * (INV_CHUNK // 2)
-                lin_ps = acc_psum.tile([P, INV_CHUNK // 2, HIDDEN], F32, tag=tag)
-                for i in range(INV_CHUNK // 2):
-                    nc.tensor.matmul_mx(
-                        out=lin_ps[:, i, :],
-                        lhsT=inv_codes[:, first + i, :].bitcast(FP8X4),
-                        lhsT_scale=inv_planes[:, first + i, :],
-                        rhs=w_codes[:, LINEAR, :].bitcast(FP8X4),
-                        rhs_scale=w_planes[:, LINEAR, :],
-                        start=True,
-                        stop=True,
-                    )
-                nc.vector.tensor_tensor(
-                    out=z_all[:, first : first + INV_CHUNK // 2, :],
-                    in0=lin_ps[:],
-                    in1=bias_rows[:].unsqueeze(1).to_broadcast([P, INV_CHUNK // 2, HIDDEN]),
-                    op=ALU.add,
-                )
-
         def load(t):
             x_sb = x_pool.tile([P, COMPONENTS, CHANNELS], BF16)
-            nc.vector.tensor_copy(
+            nc.scalar.copy(
                 out=x_sb[:, :, 0:2],
                 in_=first_channel[:, t, :].unsqueeze(2).to_broadcast([P, COMPONENTS, 2]),
             )
@@ -173,9 +159,11 @@ def tile_ryeelman_pa_t_kernel(
             nc.scalar.activation(out=squares[:, 0:2, :], in_=x_sb[:, 0:2, :], func=ACT.Square)
             nc.scalar.activation(out=squares[:, 2, :], in_=x_sb[:, 2, :], func=ACT.Square)
             two_squares = work.tile([P, CHANNELS], F32)
-            nc.gpsimd.tensor_tensor(out=two_squares[:], in0=squares[:, 0, :], in1=squares[:, 1, :], op=ALU.add)
             length2 = work.tile([P, CHANNELS], F32, bufs=3)
-            nc.gpsimd.tensor_tensor(out=length2[:], in0=two_squares[:], in1=squares[:, 2, :], op=ALU.add)
+            for g in range(PASSES):
+                half = slice(g * K_PASS, (g + 1) * K_PASS)
+                nc.gpsimd.tensor_tensor(out=two_squares[:, half], in0=squares[:, 0, half], in1=squares[:, 1, half], op=ALU.add)
+                nc.gpsimd.tensor_tensor(out=length2[:, half], in0=two_squares[:, half], in1=squares[:, 2, half], op=ALU.add)
             length2_tiles[t] = length2
 
         def inverse_lengths(t):
@@ -220,13 +208,17 @@ def tile_ryeelman_pa_t_kernel(
                     in1=factor[:].rearrange("p g b (u e) -> p (g b) u e", e=2),
                     op=ALU.mult,
                 )
-            for j in range(COMPONENTS):
-                nc.vector.quantize_mx(out=xn_codes[:, j, :].bitcast(FP8X4), scales=xn_planes[:, j, :], in_=xn[:, j, :])
+            for first, last in ((0, 2), (2, 3)):
+                nc.vector.quantize_mx(
+                    out=xn_codes[:, first:last, :].rearrange("p j c -> p (j c)").bitcast(FP8X4),
+                    scales=xn_planes[:, first:last, :].rearrange("p j c -> p (j c)"),
+                    in_=xn[:, first:last, :].rearrange("p j c -> p (j c)"),
+                )
             operand_tiles[t] = (xn_codes, xn_planes)
 
-        def project(t):
+        def multiply(t):
             xn_codes, xn_planes = operand_tiles[t]
-            left_ps = acc_psum.tile([P, COMPONENTS, HIDDEN], F32, tag="left")
+            left_ps = acc_psum.tile([P, COMPONENTS + 1, HIDDEN], F32, tag="left")
             right_ps = acc_psum.tile([P, COMPONENTS, HIDDEN], F32, tag="right")
             for side, acc in ((RIGHT, right_ps), (LEFT, left_ps)):
                 for j in range(COMPONENTS):
@@ -240,15 +232,26 @@ def tile_ryeelman_pa_t_kernel(
                             start=(g == 0),
                             stop=(g == PASSES - 1),
                         )
-            right_sb = work.tile([P, COMPONENTS, HIDDEN], F32)
-            nc.vector.tensor_copy(out=right_sb[:], in_=right_ps[:])
-            products = work.tile([P, COMPONENTS, HIDDEN], F32)
-            nc.vector.tensor_tensor(out=products[:], in0=left_ps[:], in1=right_sb[:], op=ALU.mult)
-            proj = work.tile([P, HIDDEN], F32)
-            nc.vector.tensor_reduce(
-                out=proj[:], in_=products[:].rearrange("p j h -> p h j"), axis=mybir.AxisListType.X, op=ALU.add
+            nc.tensor.matmul_mx(
+                out=left_ps[:, COMPONENTS, :],
+                lhsT=inv_codes[:, t, :].bitcast(FP8X4),
+                lhsT_scale=inv_planes[:, t, :],
+                rhs=w_codes[:, LINEAR, :].bitcast(FP8X4),
+                rhs_scale=w_planes[:, LINEAR, :],
+                start=True,
+                stop=True,
             )
-            nc.vector.tensor_tensor(out=z_all[:, t, :], in0=proj[:], in1=z_all[:, t, :], op=ALU.add)
+            product_tiles[t] = (left_ps, right_ps)
+
+        def combine(t):
+            left_ps, right_ps = product_tiles[t]
+            right_and_one = right_sets[t % 2]
+            terms = term_sets[t % 2]
+            nc.scalar.copy(out=right_and_one[:, 0:COMPONENTS, :], in_=right_ps[:])
+            nc.vector.tensor_tensor(out=terms[:, 0 : COMPONENTS + 1, :], in0=left_ps[:], in1=right_and_one[:], op=ALU.mult)
+            nc.vector.tensor_reduce(
+                out=z_all[:, t, :], in_=terms[:].rearrange("p s h -> p h s"), axis=mybir.AxisListType.X, op=ALU.add
+            )
 
         def finish(begin, end):
             nc.scalar.activation(out=z_all[:, begin:end, :], in_=z_all[:, begin:end, :], func=ACT.Tanh)
@@ -256,29 +259,28 @@ def tile_ryeelman_pa_t_kernel(
 
         for t in range(LOAD_AHEAD - 1):
             load(t)
-        load_weight(nc, w_codes, w_planes, LINEAR, W_ii_words, W_ii_scales)
         load_invariants(0)
         load(LOAD_AHEAD - 1)
-        nc.sync.dma_start(out=bias_rows[:], in_=b_ii.partition_broadcast(P))
 
         for step in range(TILES + 4):
             if step + LOAD_AHEAD < TILES:
                 load(step + LOAD_AHEAD)
-            if step % INV_PERIOD == 0 and step // INV_PERIOD + 1 < INV_CHUNKS:
-                load_invariants(step // INV_PERIOD + 1)
+            if step + 1 < INV_CHUNKS:
+                load_invariants(step + 1)
             if step == 1:
+                load_weight(nc, w_codes, w_planes, LINEAR, W_ii_words, W_ii_scales)
                 load_weight(nc, w_codes, w_planes, LEFT, W_left_words, W_left_scales)
                 load_weight(nc, w_codes, w_planes, RIGHT, W_right_words, W_right_scales)
-            if step % INV_PERIOD == 0 and step // INV_PERIOD < INV_CHUNKS:
-                quantise_invariants(step // INV_PERIOD)
-            if step % INV_PERIOD == 1 and step // INV_PERIOD < INV_CHUNKS:
-                linear(step // INV_PERIOD)
+            if step < INV_CHUNKS:
+                quantise_invariants(step)
             if 0 <= step - 3 < TILES:
                 normalise_and_quantise(step - 3)
             if 0 <= step - 4 < TILES:
-                project(step - 4)
+                multiply(step - 4)
             if step < TILES:
                 squared_lengths(step)
+            if 0 <= step - 4 < TILES:
+                combine(step - 4)
             if 0 <= step - 2 < TILES:
                 inverse_lengths(step - 2)
             if step - 4 == FIRST_STORE_TILES:

@@ -72,7 +72,8 @@ def tile_ryeelman_pa_t_kernel(
     with ExitStack() as ctx:
         keep = ctx.enter_context(tc.tile_pool(name="keep", bufs=1))
         inv_pool = ctx.enter_context(tc.tile_pool(name="inv", bufs=2))
-        x_pool = ctx.enter_context(tc.tile_pool(name="x", bufs=LOAD_AHEAD + 4))
+        raw_pool = ctx.enter_context(tc.tile_pool(name="raw", bufs=LOAD_AHEAD + 1))
+        x_pool = ctx.enter_context(tc.tile_pool(name="x", bufs=6))
         work = ctx.enter_context(tc.tile_pool(name="work", bufs=2))
         words_psum = ctx.enter_context(tc.psum_pool(name="words", bufs=4))
         lengths_psum = ctx.enter_context(tc.psum_pool(name="lengths", bufs=2))
@@ -109,6 +110,7 @@ def tile_ryeelman_pa_t_kernel(
             term_sets.append(terms)
 
         inv_tiles = {}
+        raw_tiles = {}
         x_tiles = {}
         length2_tiles = {}
         factor_tiles = {}
@@ -145,12 +147,17 @@ def tile_ryeelman_pa_t_kernel(
             )
 
         def load(t):
+            x_raw = raw_pool.tile([P, COMPONENTS, CHANNELS], BF16)
+            nc.sync.dma_start(out=x_raw[:, :, 0 : CHANNELS - 1], in_=hidden_rows[t])
+            raw_tiles[t] = x_raw
+
+        def shift(t):
             x_sb = x_pool.tile([P, COMPONENTS, CHANNELS], BF16)
             nc.scalar.copy(
                 out=x_sb[:, :, 0:2],
                 in_=first_channel[:, t, :].unsqueeze(2).to_broadcast([P, COMPONENTS, 2]),
             )
-            nc.sync.dma_start(out=x_sb[:, :, 1:CHANNELS], in_=hidden_rows[t])
+            nc.vector.tensor_copy(out=x_sb[:, :, 1:CHANNELS], in_=raw_tiles[t][:, :, 0 : CHANNELS - 1])
             x_tiles[t] = x_sb
 
         def squared_lengths(t):
@@ -261,6 +268,7 @@ def tile_ryeelman_pa_t_kernel(
             load(t)
         load_invariants(0)
         load(LOAD_AHEAD - 1)
+        shift(0)
 
         for step in range(TILES + 4):
             if step + LOAD_AHEAD < TILES:
@@ -271,6 +279,8 @@ def tile_ryeelman_pa_t_kernel(
                 load_weight(nc, w_codes, w_planes, LINEAR, W_ii_words, W_ii_scales)
                 load_weight(nc, w_codes, w_planes, LEFT, W_left_words, W_left_scales)
                 load_weight(nc, w_codes, w_planes, RIGHT, W_right_words, W_right_scales)
+            if step + 1 < TILES:
+                shift(step + 1)
             if step < INV_CHUNKS:
                 quantise_invariants(step)
             if 0 <= step - 3 < TILES:

@@ -64,7 +64,7 @@ def tile_ryeelman_pa_t_kernel(
     out,
 ):
     nc = tc.nc
-    hidden_rows = equivariant_hidden.rearrange("(p t) j c -> t p j c", t=TILES)
+    hidden_runs = equivariant_hidden.rearrange("(p t) j c -> p (t j c)", t=TILES)
     inv_input_rows = invariant_input.rearrange("(p t) k -> p t k", t=TILES)
     inv_hidden_rows = invariant_hidden.rearrange("(p t) k -> p t k", t=TILES)
     out_rows = out.rearrange("(p t) h -> p t h", t=TILES)
@@ -72,8 +72,7 @@ def tile_ryeelman_pa_t_kernel(
     with ExitStack() as ctx:
         keep = ctx.enter_context(tc.tile_pool(name="keep", bufs=1))
         inv_pool = ctx.enter_context(tc.tile_pool(name="inv", bufs=2))
-        raw_pool = ctx.enter_context(tc.tile_pool(name="raw", bufs=LOAD_AHEAD + 1))
-        x_pool = ctx.enter_context(tc.tile_pool(name="x", bufs=6))
+        x_pool = ctx.enter_context(tc.tile_pool(name="x", bufs=LOAD_AHEAD + 4))
         work = ctx.enter_context(tc.tile_pool(name="work", bufs=2))
         words_psum = ctx.enter_context(tc.psum_pool(name="words", bufs=4))
         lengths_psum = ctx.enter_context(tc.psum_pool(name="lengths", bufs=2))
@@ -110,7 +109,6 @@ def tile_ryeelman_pa_t_kernel(
             term_sets.append(terms)
 
         inv_tiles = {}
-        raw_tiles = {}
         x_tiles = {}
         length2_tiles = {}
         factor_tiles = {}
@@ -147,21 +145,21 @@ def tile_ryeelman_pa_t_kernel(
             )
 
         def load(t):
-            x_raw = raw_pool.tile([P, COMPONENTS, CHANNELS], BF16)
-            nc.sync.dma_start(out=x_raw[:, :, 0 : CHANNELS - 1], in_=hidden_rows[t])
-            raw_tiles[t] = x_raw
-
-        def shift(t):
             x_sb = x_pool.tile([P, COMPONENTS, CHANNELS], BF16)
-            nc.scalar.copy(
-                out=x_sb[:, :, 0:2],
-                in_=first_channel[:, t, :].unsqueeze(2).to_broadcast([P, COMPONENTS, 2]),
-            )
-            nc.vector.tensor_copy(out=x_sb[:, :, 1:CHANNELS], in_=raw_tiles[t][:, :, 0 : CHANNELS - 1])
+            for j in range(COMPONENTS):
+                first = (t * COMPONENTS + j) * (CHANNELS - 1)
+                if first == 0:
+                    row_raw = keep.tile([P, 8 + CHANNELS], BF16)
+                    nc.vector.memset(row_raw[:, 0:8], 0.0)
+                    nc.sync.dma_start(out=row_raw[:, 8 : 8 + CHANNELS - 1], in_=hidden_runs[:, 0 : CHANNELS - 1])
+                    nc.vector.tensor_copy(out=x_sb[:, j, :], in_=row_raw[:, 7 : 7 + CHANNELS])
+                else:
+                    nc.sync.dma_start(out=x_sb[:, j, :], in_=hidden_runs[:, first - 1 : first - 1 + CHANNELS])
             x_tiles[t] = x_sb
 
         def squared_lengths(t):
             x_sb = x_tiles[t]
+            nc.scalar.copy(out=x_sb[:, :, 0:1], in_=first_channel[:, t, :].unsqueeze(2))
             squares = work.tile([P, COMPONENTS, CHANNELS], F32)
             nc.scalar.activation(out=squares[:, 0:2, :], in_=x_sb[:, 0:2, :], func=ACT.Square)
             nc.scalar.activation(out=squares[:, 2, :], in_=x_sb[:, 2, :], func=ACT.Square)
@@ -268,7 +266,6 @@ def tile_ryeelman_pa_t_kernel(
             load(t)
         load_invariants(0)
         load(LOAD_AHEAD - 1)
-        shift(0)
 
         for step in range(TILES + 4):
             if step + LOAD_AHEAD < TILES:
@@ -279,8 +276,6 @@ def tile_ryeelman_pa_t_kernel(
                 load_weight(nc, w_codes, w_planes, LINEAR, W_ii_words, W_ii_scales)
                 load_weight(nc, w_codes, w_planes, LEFT, W_left_words, W_left_scales)
                 load_weight(nc, w_codes, w_planes, RIGHT, W_right_words, W_right_scales)
-            if step + 1 < TILES:
-                shift(step + 1)
             if step < INV_CHUNKS:
                 quantise_invariants(step)
             if 0 <= step - 3 < TILES:

@@ -98,15 +98,13 @@ def tile_ryeelman_pa_t_kernel(
         inv_codes = keep.tile([P, TILES, P], U32, align_bytes=64)
         inv_planes = keep.tile([P, TILES, P], U8, align_bytes=64)
         z_all = keep.tile([P, TILES, HIDDEN], F32)
+        bias_f32 = keep.tile([P, HIDDEN], F32)
+        nc.vector.tensor_copy(out=bias_f32[:], in_=bias_rows[:])
         right_sets = []
-        term_sets = []
         for parity in range(2):
             right_and_one = keep.tile([P, COMPONENTS + 1, HIDDEN], F32, name="right_and_one%d" % parity)
             nc.vector.memset(right_and_one[:, COMPONENTS, :], 1.0)
             right_sets.append(right_and_one)
-            terms = keep.tile([P, COMPONENTS + 2, HIDDEN], F32, name="terms%d" % parity)
-            nc.vector.tensor_copy(out=terms[:, COMPONENTS + 1, :], in_=bias_rows[:])
-            term_sets.append(terms)
 
         inv_tiles = {}
         x_tiles = {}
@@ -160,26 +158,34 @@ def tile_ryeelman_pa_t_kernel(
         def squared_lengths(t):
             x_sb = x_tiles[t]
             nc.scalar.copy(out=x_sb[:, :, 0:1], in_=first_channel[:, t, :].unsqueeze(2))
-            squares = work.tile([P, COMPONENTS, CHANNELS], F32)
-            nc.scalar.activation(out=squares[:, 0:2, :], in_=x_sb[:, 0:2, :], func=ACT.Square)
-            nc.scalar.activation(out=squares[:, 2, :], in_=x_sb[:, 2, :], func=ACT.Square)
-            two_squares = work.tile([P, CHANNELS], F32)
-            length2 = work.tile([P, CHANNELS], F32, bufs=3)
-            for g in range(PASSES):
-                half = slice(g * K_PASS, (g + 1) * K_PASS)
-                nc.gpsimd.tensor_tensor(out=two_squares[:, half], in0=squares[:, 0, half], in1=squares[:, 1, half], op=ALU.add)
-                nc.gpsimd.tensor_tensor(out=length2[:, half], in0=two_squares[:, half], in1=squares[:, 2, half], op=ALU.add)
-            length2_tiles[t] = length2
+            squares = work.tile([P, COMPONENTS * PASSES, PACK, P], F32, bufs=3)
+            x_halves = x_sb[:].rearrange("p j (g c) -> p (j g) c", g=PASSES)
+            on_scalar = 2 * PASSES
+            nc.scalar.activation(
+                out=squares[:, 0:on_scalar],
+                in_=x_halves[:, 0:on_scalar, :].rearrange("p a (q k) -> p a k q", k=PACK),
+                func=ACT.Square,
+            )
+            for a in range(on_scalar, COMPONENTS * PASSES):
+                stepped = x_halves[:, a, :].rearrange("p (q k) -> p k q", k=PACK)
+                nc.gpsimd.tensor_tensor(out=squares[:, a], in0=stepped, in1=stepped, op=ALU.mult)
+            length2_tiles[t] = squares
 
         def inverse_lengths(t):
-            length2 = length2_tiles[t]
+            squares = length2_tiles[t]
             inv_length = work.tile([P, PASSES, P, PACK], F32)
             for g in range(PASSES):
                 length2T = lengths_psum.tile([P, PACK, P], F32)
                 for k in range(PACK):
-                    nc.tensor.transpose(
-                        length2T[:, k, :], length2[:, g * K_PASS + k : (g + 1) * K_PASS : PACK], identity[:]
-                    )
+                    for j in range(COMPONENTS):
+                        nc.tensor.matmul(
+                            out=length2T[:, k, :],
+                            lhsT=squares[:, PASSES * j + g, k, :],
+                            rhs=identity[:],
+                            is_transpose=True,
+                            start=(j == 0),
+                            stop=(j == COMPONENTS - 1),
+                        )
                 nc.scalar.activation(
                     out=inv_length[:, g],
                     in_=length2T[:].rearrange("p k b -> p b k"),
@@ -251,12 +257,14 @@ def tile_ryeelman_pa_t_kernel(
         def combine(t):
             left_ps, right_ps = product_tiles[t]
             right_and_one = right_sets[t % 2]
-            terms = term_sets[t % 2]
+            terms = work.tile([P, COMPONENTS + 1, HIDDEN], F32)
             nc.scalar.copy(out=right_and_one[:, 0:COMPONENTS, :], in_=right_ps[:])
-            nc.vector.tensor_tensor(out=terms[:, 0 : COMPONENTS + 1, :], in0=left_ps[:], in1=right_and_one[:], op=ALU.mult)
-            nc.vector.tensor_reduce(
-                out=z_all[:, t, :], in_=terms[:].rearrange("p s h -> p h s"), axis=mybir.AxisListType.X, op=ALU.add
-            )
+            nc.vector.tensor_tensor(out=terms[:], in0=left_ps[:], in1=right_and_one[:], op=ALU.mult)
+            pair_sums = work.tile([P, 2, HIDDEN], F32)
+            nc.gpsimd.tensor_tensor(out=pair_sums[:], in0=terms[:, 0:2, :], in1=terms[:, 2:4, :], op=ALU.add)
+            with_bias = work.tile([P, HIDDEN], F32)
+            nc.gpsimd.tensor_tensor(out=with_bias[:], in0=pair_sums[:, 0, :], in1=bias_f32[:], op=ALU.add)
+            nc.gpsimd.tensor_tensor(out=z_all[:, t, :], in0=with_bias[:], in1=pair_sums[:, 1, :], op=ALU.add)
 
         def finish(begin, end):
             nc.scalar.activation(out=z_all[:, begin:end, :], in_=z_all[:, begin:end, :], func=ACT.Tanh)

@@ -27,7 +27,8 @@ TILES = BATCH // P
 INV_CHUNK = 8
 INV_CHUNKS = TILES // INV_CHUNK
 LOAD_AHEAD = 3
-FIRST_STORE_TILES = 24
+SUM_GROUP = 4
+SCALAR_COMPONENTS = 2
 
 LEFT, RIGHT, LINEAR = 0, 2, 4
 WEIGHT_SLOTS = 5
@@ -74,9 +75,10 @@ def tile_ryeelman_pa_t_kernel(
         inv_pool = ctx.enter_context(tc.tile_pool(name="inv", bufs=2))
         x_pool = ctx.enter_context(tc.tile_pool(name="x", bufs=LOAD_AHEAD + 4))
         work = ctx.enter_context(tc.tile_pool(name="work", bufs=2))
-        words_psum = ctx.enter_context(tc.psum_pool(name="words", bufs=4))
+        words_psum = ctx.enter_context(tc.psum_pool(name="words", bufs=3))
         lengths_psum = ctx.enter_context(tc.psum_pool(name="lengths", bufs=2))
         acc_psum = ctx.enter_context(tc.psum_pool(name="acc", bufs=1))
+        sum_psum = ctx.enter_context(tc.psum_pool(name="sums", bufs=1))
         ctx.enter_context(tc.manual_schedule())
 
         first_channel = keep.tile([P, TILES, COMPONENTS], BF16)
@@ -94,24 +96,27 @@ def tile_ryeelman_pa_t_kernel(
         make_identity(nc, identity[:])
         bias_rows = keep.tile([P, HIDDEN], BF16)
         nc.sync.dma_start(out=bias_rows[:], in_=b_ii.partition_broadcast(P))
+        bias_column = keep.tile([P, 1], F32)
 
         inv_codes = keep.tile([P, TILES, P], U32, align_bytes=64)
         inv_planes = keep.tile([P, TILES, P], U8, align_bytes=64)
         z_all = keep.tile([P, TILES, HIDDEN], F32)
-        bias_f32 = keep.tile([P, HIDDEN], F32)
-        nc.vector.tensor_copy(out=bias_f32[:], in_=bias_rows[:])
-        right_sets = []
-        for parity in range(2):
-            right_and_one = keep.tile([P, COMPONENTS + 1, HIDDEN], F32, name="right_and_one%d" % parity)
-            nc.vector.memset(right_and_one[:, COMPONENTS, :], 1.0)
-            right_sets.append(right_and_one)
 
         inv_tiles = {}
         x_tiles = {}
-        length2_tiles = {}
+        square_tiles = {}
         factor_tiles = {}
         operand_tiles = {}
         product_tiles = {}
+        term_tiles = {}
+        sum_tiles = {}
+
+        def bias_to_partitions():
+            bias_f32 = keep.tile([P, HIDDEN], F32)
+            nc.vector.tensor_copy(out=bias_f32[:], in_=bias_rows[:])
+            biasT = lengths_psum.tile([P, PACK, P], F32, tag="length2T")
+            nc.tensor.transpose(biasT[:, 0, :], bias_f32[:], identity[:])
+            nc.vector.tensor_copy(out=bias_column[:], in_=biasT[:, 0, 0:1])
 
         def load_invariants(chunk):
             first = chunk * INV_CHUNK
@@ -155,32 +160,38 @@ def tile_ryeelman_pa_t_kernel(
                     nc.sync.dma_start(out=x_sb[:, j, :], in_=hidden_runs[:, first - 1 : first - 1 + CHANNELS])
             x_tiles[t] = x_sb
 
-        def squared_lengths(t):
-            x_sb = x_tiles[t]
-            nc.scalar.copy(out=x_sb[:, :, 0:1], in_=first_channel[:, t, :].unsqueeze(2))
-            squares = work.tile([P, COMPONENTS * PASSES, PACK, P], F32, bufs=3)
-            x_halves = x_sb[:].rearrange("p j (g c) -> p (j g) c", g=PASSES)
-            on_scalar = 2 * PASSES
-            nc.scalar.activation(
-                out=squares[:, 0:on_scalar],
-                in_=x_halves[:, 0:on_scalar, :].rearrange("p a (q k) -> p a k q", k=PACK),
-                func=ACT.Square,
-            )
-            for a in range(on_scalar, COMPONENTS * PASSES):
-                stepped = x_halves[:, a, :].rearrange("p (q k) -> p k q", k=PACK)
-                nc.gpsimd.tensor_tensor(out=squares[:, a], in0=stepped, in1=stepped, op=ALU.mult)
-            length2_tiles[t] = squares
+        def stepped_halves(t):
+            halves = x_tiles[t][:].rearrange("p j (g c) -> p (j g) c", g=PASSES)
+            return halves.rearrange("p a (q k) -> p a k q", k=PACK)
+
+        def squares_on_gpsimd(t):
+            nc.vector.tensor_copy(out=x_tiles[t][:, :, 0:1], in_=first_channel[:, t, :].unsqueeze(2))
+            stepped = stepped_halves(t)
+            late = work.tile([P, (COMPONENTS - SCALAR_COMPONENTS) * PASSES, PACK, P], F32, bufs=4)
+            for a in range((COMPONENTS - SCALAR_COMPONENTS) * PASSES):
+                source = stepped[:, SCALAR_COMPONENTS * PASSES + a]
+                nc.gpsimd.tensor_tensor(out=late[:, a], in0=source, in1=source, op=ALU.mult)
+            square_tiles[t] = [None, late]
+
+        def squares_on_scalar(t):
+            early = work.tile([P, SCALAR_COMPONENTS * PASSES, PACK, P], F32, bufs=3)
+            nc.scalar.activation(out=early[:], in_=stepped_halves(t)[:, 0 : SCALAR_COMPONENTS * PASSES], func=ACT.Square)
+            square_tiles[t][0] = early
 
         def inverse_lengths(t):
-            squares = length2_tiles[t]
+            early, late = square_tiles[t]
             inv_length = work.tile([P, PASSES, P, PACK], F32)
             for g in range(PASSES):
-                length2T = lengths_psum.tile([P, PACK, P], F32)
+                length2T = lengths_psum.tile([P, PACK, P], F32, tag="length2T")
                 for k in range(PACK):
                     for j in range(COMPONENTS):
+                        if j < SCALAR_COMPONENTS:
+                            source = early[:, PASSES * j + g, k, :]
+                        else:
+                            source = late[:, PASSES * (j - SCALAR_COMPONENTS) + g, k, :]
                         nc.tensor.matmul(
                             out=length2T[:, k, :],
-                            lhsT=squares[:, PASSES * j + g, k, :],
+                            lhsT=source,
                             rhs=identity[:],
                             is_transpose=True,
                             start=(j == 0),
@@ -229,42 +240,61 @@ def tile_ryeelman_pa_t_kernel(
 
         def multiply(t):
             xn_codes, xn_planes = operand_tiles[t]
-            left_ps = acc_psum.tile([P, COMPONENTS + 1, HIDDEN], F32, tag="left")
-            right_ps = acc_psum.tile([P, COMPONENTS, HIDDEN], F32, tag="right")
+            right_ps = acc_psum.tile([P, COMPONENTS + 1, P], F32, tag="right")
+            left_ps = acc_psum.tile([P, COMPONENTS + 1, P], F32, tag="left")
             for side, acc in ((RIGHT, right_ps), (LEFT, left_ps)):
                 for j in range(COMPONENTS):
                     for g in range(PASSES):
                         nc.tensor.matmul_mx(
                             out=acc[:, j, :],
-                            lhsT=xn_codes[:, j, g * P : (g + 1) * P].bitcast(FP8X4),
-                            lhsT_scale=xn_planes[:, j, g * P : (g + 1) * P],
-                            rhs=w_codes[:, side + g, :].bitcast(FP8X4),
-                            rhs_scale=w_planes[:, side + g, :],
+                            lhsT=w_codes[:, side + g, :].bitcast(FP8X4),
+                            lhsT_scale=w_planes[:, side + g, :],
+                            rhs=xn_codes[:, j, g * P : (g + 1) * P].bitcast(FP8X4),
+                            rhs_scale=xn_planes[:, j, g * P : (g + 1) * P],
                             start=(g == 0),
                             stop=(g == PASSES - 1),
                         )
-            nc.tensor.matmul_mx(
-                out=left_ps[:, COMPONENTS, :],
-                lhsT=inv_codes[:, t, :].bitcast(FP8X4),
-                lhsT_scale=inv_planes[:, t, :],
-                rhs=w_codes[:, LINEAR, :].bitcast(FP8X4),
-                rhs_scale=w_planes[:, LINEAR, :],
-                start=True,
-                stop=True,
-            )
+                if side == RIGHT:
+                    nc.tensor.matmul_mx(
+                        out=right_ps[:, COMPONENTS, :],
+                        lhsT=w_codes[:, LINEAR, :].bitcast(FP8X4),
+                        lhsT_scale=w_planes[:, LINEAR, :],
+                        rhs=inv_codes[:, t, :].bitcast(FP8X4),
+                        rhs_scale=inv_planes[:, t, :],
+                        start=True,
+                        stop=True,
+                    )
             product_tiles[t] = (left_ps, right_ps)
 
         def combine(t):
             left_ps, right_ps = product_tiles[t]
-            right_and_one = right_sets[t % 2]
-            terms = work.tile([P, COMPONENTS + 1, HIDDEN], F32)
-            nc.scalar.copy(out=right_and_one[:, 0:COMPONENTS, :], in_=right_ps[:])
-            nc.vector.tensor_tensor(out=terms[:], in0=left_ps[:], in1=right_and_one[:], op=ALU.mult)
-            pair_sums = work.tile([P, 2, HIDDEN], F32)
-            nc.gpsimd.tensor_tensor(out=pair_sums[:], in0=terms[:, 0:2, :], in1=terms[:, 2:4, :], op=ALU.add)
-            with_bias = work.tile([P, HIDDEN], F32)
-            nc.gpsimd.tensor_tensor(out=with_bias[:], in0=pair_sums[:, 0, :], in1=bias_f32[:], op=ALU.add)
-            nc.gpsimd.tensor_tensor(out=z_all[:, t, :], in0=with_bias[:], in1=pair_sums[:, 1, :], op=ALU.add)
+            right_sb = work.tile([P, COMPONENTS, P], F32)
+            terms = work.tile([P, COMPONENTS + 1, P], F32)
+            nc.scalar.copy(out=right_sb[:], in_=right_ps[:, 0:COMPONENTS, :])
+            nc.scalar.activation(
+                out=terms[:, COMPONENTS, :], in_=right_ps[:, COMPONENTS, :], func=ACT.Identity, bias=bias_column[:], scale=1.0
+            )
+            nc.vector.tensor_tensor(
+                out=terms[:, 0:COMPONENTS, :], in0=left_ps[:, 0:COMPONENTS, :], in1=right_sb[:], op=ALU.mult
+            )
+            term_tiles[t] = terms
+
+        def add_up(t):
+            if t % SUM_GROUP == 0:
+                sum_tiles[t // SUM_GROUP] = sum_psum.tile([P, SUM_GROUP, HIDDEN], F32, name="sums")
+            sums = sum_tiles[t // SUM_GROUP]
+            for s in range(COMPONENTS + 1):
+                nc.tensor.matmul(
+                    out=sums[:, t % SUM_GROUP, :],
+                    lhsT=term_tiles[t][:, s, :],
+                    rhs=identity[:],
+                    is_transpose=True,
+                    start=(s == 0),
+                    stop=(s == COMPONENTS),
+                )
+
+        def collect(group):
+            nc.scalar.copy(out=z_all[:, group * SUM_GROUP : (group + 1) * SUM_GROUP, :], in_=sum_tiles[group][:])
 
         def finish(begin, end):
             nc.scalar.activation(out=z_all[:, begin:end, :], in_=z_all[:, begin:end, :], func=ACT.Tanh)
@@ -274,8 +304,11 @@ def tile_ryeelman_pa_t_kernel(
             load(t)
         load_invariants(0)
         load(LOAD_AHEAD - 1)
+        squares_on_gpsimd(0)
 
-        for step in range(TILES + 4):
+        last_group = TILES // SUM_GROUP - 1
+        early_tiles = last_group * SUM_GROUP
+        for step in range(TILES + 6):
             if step + LOAD_AHEAD < TILES:
                 load(step + LOAD_AHEAD)
             if step + 1 < INV_CHUNKS:
@@ -284,18 +317,28 @@ def tile_ryeelman_pa_t_kernel(
                 load_weight(nc, w_codes, w_planes, LINEAR, W_ii_words, W_ii_scales)
                 load_weight(nc, w_codes, w_planes, LEFT, W_left_words, W_left_scales)
                 load_weight(nc, w_codes, w_planes, RIGHT, W_right_words, W_right_scales)
+                bias_to_partitions()
             if step < INV_CHUNKS:
                 quantise_invariants(step)
+            if 0 <= step - 2 < TILES:
+                inverse_lengths(step - 2)
             if 0 <= step - 3 < TILES:
                 normalise_and_quantise(step - 3)
+            if step + 1 < TILES:
+                squares_on_gpsimd(step + 1)
+            if 0 <= step - 5 < TILES:
+                add_up(step - 5)
             if 0 <= step - 4 < TILES:
                 multiply(step - 4)
             if step < TILES:
-                squared_lengths(step)
+                squares_on_scalar(step)
             if 0 <= step - 4 < TILES:
                 combine(step - 4)
-            if 0 <= step - 2 < TILES:
-                inverse_lengths(step - 2)
-            if step - 4 == FIRST_STORE_TILES:
-                finish(0, FIRST_STORE_TILES)
-        finish(FIRST_STORE_TILES, TILES)
+            if 0 <= step - 5 < early_tiles and (step - 5) % SUM_GROUP == SUM_GROUP - 1:
+                collect((step - 5) // SUM_GROUP)
+            pieces = 3
+            piece = step - (TILES + 1)
+            if 0 <= piece < pieces:
+                finish(early_tiles * piece // pieces, early_tiles * (piece + 1) // pieces)
+        nc.scalar.activation(out=z_all[:, early_tiles:TILES, :], in_=sum_tiles[last_group][:], func=ACT.Tanh)
+        nc.sync.dma_start(out=out_rows[:, early_tiles:TILES, :], in_=z_all[:, early_tiles:TILES, :])

@@ -28,7 +28,8 @@ INV_CHUNK = 8
 INV_CHUNKS = TILES // INV_CHUNK
 LOAD_AHEAD = 3
 SUM_GROUP = 4
-SCALAR_COMPONENTS = 2
+HALVES = COMPONENTS * PASSES
+SCALAR_HALVES = 3
 
 LEFT, RIGHT, LINEAR = 0, 2, 4
 WEIGHT_SLOTS = 5
@@ -167,15 +168,15 @@ def tile_ryeelman_pa_t_kernel(
         def squares_on_gpsimd(t):
             nc.vector.tensor_copy(out=x_tiles[t][:, :, 0:1], in_=first_channel[:, t, :].unsqueeze(2))
             stepped = stepped_halves(t)
-            late = work.tile([P, (COMPONENTS - SCALAR_COMPONENTS) * PASSES, PACK, P], F32, bufs=4)
-            for a in range((COMPONENTS - SCALAR_COMPONENTS) * PASSES):
-                source = stepped[:, SCALAR_COMPONENTS * PASSES + a]
+            late = work.tile([P, HALVES - SCALAR_HALVES, PACK, P], F32, bufs=4)
+            for a in range(HALVES - SCALAR_HALVES):
+                source = stepped[:, SCALAR_HALVES + a]
                 nc.gpsimd.tensor_tensor(out=late[:, a], in0=source, in1=source, op=ALU.mult)
             square_tiles[t] = [None, late]
 
         def squares_on_scalar(t):
-            early = work.tile([P, SCALAR_COMPONENTS * PASSES, PACK, P], F32, bufs=3)
-            nc.scalar.activation(out=early[:], in_=stepped_halves(t)[:, 0 : SCALAR_COMPONENTS * PASSES], func=ACT.Square)
+            early = work.tile([P, SCALAR_HALVES, PACK, P], F32, bufs=3)
+            nc.scalar.activation(out=early[:], in_=stepped_halves(t)[:, 0:SCALAR_HALVES], func=ACT.Square)
             square_tiles[t][0] = early
 
         def inverse_lengths(t):
@@ -185,10 +186,11 @@ def tile_ryeelman_pa_t_kernel(
                 length2T = lengths_psum.tile([P, PACK, P], F32, tag="length2T")
                 for k in range(PACK):
                     for j in range(COMPONENTS):
-                        if j < SCALAR_COMPONENTS:
-                            source = early[:, PASSES * j + g, k, :]
+                        half = PASSES * j + g
+                        if half < SCALAR_HALVES:
+                            source = early[:, half, k, :]
                         else:
-                            source = late[:, PASSES * (j - SCALAR_COMPONENTS) + g, k, :]
+                            source = late[:, half - SCALAR_HALVES, k, :]
                         nc.tensor.matmul(
                             out=length2T[:, k, :],
                             lhsT=source,

@@ -30,6 +30,8 @@ LOAD_AHEAD = 3
 SUM_GROUP = 4
 HALVES = COMPONENTS * PASSES
 SCALAR_HALVES = 3
+VECTOR_HALVES = 1
+GPSIMD_FIRST = SCALAR_HALVES + VECTOR_HALVES
 
 LEFT, RIGHT, LINEAR = 0, 2, 4
 WEIGHT_SLOTS = 5
@@ -166,12 +168,13 @@ def tile_ryeelman_pa_t_kernel(
             return halves.rearrange("p a (q k) -> p a k q", k=PACK)
 
         def squares_on_gpsimd(t):
-            nc.vector.tensor_copy(out=x_tiles[t][:, :, 0:1], in_=first_channel[:, t, :].unsqueeze(2))
             stepped = stepped_halves(t)
             late = work.tile([P, HALVES - SCALAR_HALVES, PACK, P], F32, bufs=4)
-            for a in range(HALVES - SCALAR_HALVES):
-                source = stepped[:, SCALAR_HALVES + a]
-                nc.gpsimd.tensor_tensor(out=late[:, a], in0=source, in1=source, op=ALU.mult)
+            for a in range(SCALAR_HALVES, GPSIMD_FIRST):
+                nc.vector.tensor_tensor(out=late[:, a - SCALAR_HALVES], in0=stepped[:, a], in1=stepped[:, a], op=ALU.mult)
+            nc.vector.tensor_copy(out=x_tiles[t][:, :, 0:1], in_=first_channel[:, t, :].unsqueeze(2))
+            for a in range(GPSIMD_FIRST, HALVES):
+                nc.gpsimd.tensor_tensor(out=late[:, a - SCALAR_HALVES], in0=stepped[:, a], in1=stepped[:, a], op=ALU.mult)
             square_tiles[t] = [None, late]
 
         def squares_on_scalar(t):
@@ -320,14 +323,14 @@ def tile_ryeelman_pa_t_kernel(
                 load_weight(nc, w_codes, w_planes, LEFT, W_left_words, W_left_scales)
                 load_weight(nc, w_codes, w_planes, RIGHT, W_right_words, W_right_scales)
                 bias_to_partitions()
-            if step < INV_CHUNKS:
-                quantise_invariants(step)
             if 0 <= step - 2 < TILES:
                 inverse_lengths(step - 2)
             if 0 <= step - 3 < TILES:
                 normalise_and_quantise(step - 3)
             if step + 1 < TILES:
                 squares_on_gpsimd(step + 1)
+            if step < INV_CHUNKS:
+                quantise_invariants(step)
             if 0 <= step - 5 < TILES:
                 add_up(step - 5)
             if 0 <= step - 4 < TILES:

@@ -26,6 +26,12 @@ PASSES = CHANNELS // K_PASS
 TILES = BATCH // P
 INV_CHUNK = 8
 INV_CHUNKS = TILES // INV_CHUNK
+INV_ON_SCALAR = True
+INV_T = [2, 3, 4, 5]
+INV_Q = [3, 4, 5, 6]
+INV_L = [0,1,2,3]
+F_LATE = False
+SC_FIRST = False
 LOAD_AHEAD = 3
 SUM_GROUP = 4
 HALVES = COMPONENTS * PASSES
@@ -130,10 +136,12 @@ def tile_ryeelman_pa_t_kernel(
             )
             inv_tiles[chunk] = inv_sb
 
-        def quantise_invariants(chunk):
-            first = chunk * INV_CHUNK
+        grouped_tiles = {}
+
+        def group_invariants(chunk):
             inv_sb = inv_tiles[chunk]
             inv_grouped = inv_pool.tile([P, INV_CHUNK * P, PACK], BF16, align_bytes=64)
+            grouped_tiles[chunk] = inv_grouped
             for pair in range(INV_CHUNK // 2):
                 invT = words_psum.tile([P, 2, 2 * P], F32, tag="xT")
                 for i in range(2):
@@ -143,7 +151,14 @@ def tile_ryeelman_pa_t_kernel(
                             invT[:, u, i * P : (i + 1) * P], inv_words[:, u : FEATURES // 2 : 2], identity[:]
                         )
                 grouped_words = inv_grouped[:, 2 * pair * P : 2 * (pair + 1) * P, :].bitcast(F32)
-                nc.vector.tensor_copy(out=grouped_words, in_=invT[:].rearrange("p u c -> p c u"))
+                if INV_ON_SCALAR:
+                    nc.scalar.copy(out=grouped_words, in_=invT[:].rearrange("p u c -> p c u"))
+                else:
+                    nc.vector.tensor_copy(out=grouped_words, in_=invT[:].rearrange("p u c -> p c u"))
+
+        def quantise_invariants(chunk):
+            first = chunk * INV_CHUNK
+            inv_grouped = grouped_tiles[chunk]
             nc.vector.quantize_mx(
                 out=inv_codes[:, first : first + INV_CHUNK, :].rearrange("p i b -> p (i b)").bitcast(FP8X4),
                 scales=inv_planes[:, first : first + INV_CHUNK, :].rearrange("p i b -> p (i b)"),
@@ -209,6 +224,10 @@ def tile_ryeelman_pa_t_kernel(
                     bias=epsilon[:],
                     scale=1.0,
                 )
+            factor_tiles[t] = inv_length
+
+        def square_factor(t):
+            inv_length = factor_tiles[t]
             factor = work.tile([P, PASSES, P, PACK], F32)
             nc.scalar.activation(out=factor[:], in_=inv_length[:], func=ACT.Square)
             factor_tiles[t] = factor
@@ -307,7 +326,9 @@ def tile_ryeelman_pa_t_kernel(
 
         for t in range(LOAD_AHEAD - 1):
             load(t)
-        load_invariants(0)
+        for c in range(INV_CHUNKS):
+            if INV_L[c] == 0:
+                load_invariants(c)
         load(LOAD_AHEAD - 1)
         squares_on_gpsimd(0)
 
@@ -316,27 +337,41 @@ def tile_ryeelman_pa_t_kernel(
         for step in range(TILES + 6):
             if step + LOAD_AHEAD < TILES:
                 load(step + LOAD_AHEAD)
-            if step + 1 < INV_CHUNKS:
-                load_invariants(step + 1)
+            for c in range(INV_CHUNKS):
+                if INV_L[c] and step + 1 == INV_L[c]:
+                    load_invariants(c)
             if step == 1:
                 load_weight(nc, w_codes, w_planes, LINEAR, W_ii_words, W_ii_scales)
                 load_weight(nc, w_codes, w_planes, LEFT, W_left_words, W_left_scales)
                 load_weight(nc, w_codes, w_planes, RIGHT, W_right_words, W_right_scales)
                 bias_to_partitions()
+            if SC_FIRST and step < TILES:
+                squares_on_scalar(step)
             if 0 <= step - 2 < TILES:
                 inverse_lengths(step - 2)
+                if not F_LATE:
+                    square_factor(step - 2)
             if 0 <= step - 3 < TILES:
                 normalise_and_quantise(step - 3)
             if step + 1 < TILES:
                 squares_on_gpsimd(step + 1)
-            if step < INV_CHUNKS:
-                quantise_invariants(step)
+            for c in range(INV_CHUNKS):
+                if not INV_ON_SCALAR and step == INV_T[c]:
+                    group_invariants(c)
+            for c in range(INV_CHUNKS):
+                if step == INV_Q[c]:
+                    quantise_invariants(c)
             if 0 <= step - 5 < TILES:
                 add_up(step - 5)
             if 0 <= step - 4 < TILES:
                 multiply(step - 4)
-            if step < TILES:
+            if not SC_FIRST and step < TILES:
                 squares_on_scalar(step)
+            if F_LATE and 0 <= step - 2 < TILES:
+                square_factor(step - 2)
+            for c in range(INV_CHUNKS):
+                if INV_ON_SCALAR and step == INV_T[c]:
+                    group_invariants(c)
             if 0 <= step - 4 < TILES:
                 combine(step - 4)
             if 0 <= step - 5 < early_tiles and (step - 5) % SUM_GROUP == SUM_GROUP - 1:

@@ -24,20 +24,35 @@ PACK = 4
 K_PASS = P * PACK
 PASSES = CHANNELS // K_PASS
 TILES = BATCH // P
-INV_CHUNK = 8
-INV_CHUNKS = TILES // INV_CHUNK
-INV_ON_SCALAR = True
-INV_T = [2, 3, 4, 5]
-INV_Q = [3, 4, 5, 6]
-INV_L = [0,1,2,3]
-F_LATE = False
-SC_FIRST = False
-LOAD_AHEAD = 3
-SUM_GROUP = 4
+PAIRS = TILES // 2
+QUAD = 4
+QUADS = TILES // QUAD
+LOAD_AHEAD = 4
 HALVES = COMPONENTS * PASSES
 SCALAR_HALVES = 3
 VECTOR_HALVES = 1
 GPSIMD_FIRST = SCALAR_HALVES + VECTOR_HALVES
+WORDS = 3
+LENGTHS = 2
+SQA = 1
+QS = 5
+MXS = 7
+CPS = 8
+MUS = 8
+ADS = 10
+COS = 10
+CP_LATE = False
+CO_MID = True
+SUMS_IN_ACC = True
+CB = -1
+LAST = 0
+INV_L = [0, 1, 2, 3, 4, 5, 6, 7]
+INV_T = [1, 3, 5, 7, 9, 11, 13, 15]
+INV_Q = [2, 4, 6, 8, 10, 12, 14, 16]
+LIN = [7, 9, 11, 13, 15, 17, 19, 21]
+F_LATE = False
+X_FIRST = False
+ADD_FIRST = False
 
 LEFT, RIGHT, LINEAR = 0, 2, 4
 WEIGHT_SLOTS = 5
@@ -81,13 +96,12 @@ def tile_ryeelman_pa_t_kernel(
 
     with ExitStack() as ctx:
         keep = ctx.enter_context(tc.tile_pool(name="keep", bufs=1))
-        inv_pool = ctx.enter_context(tc.tile_pool(name="inv", bufs=2))
+        inv_pool = ctx.enter_context(tc.tile_pool(name="inv", bufs=3))
         x_pool = ctx.enter_context(tc.tile_pool(name="x", bufs=LOAD_AHEAD + 4))
         work = ctx.enter_context(tc.tile_pool(name="work", bufs=2))
-        words_psum = ctx.enter_context(tc.psum_pool(name="words", bufs=3))
-        lengths_psum = ctx.enter_context(tc.psum_pool(name="lengths", bufs=2))
+        words_psum = ctx.enter_context(tc.psum_pool(name="words", bufs=WORDS))
+        lengths_psum = ctx.enter_context(tc.psum_pool(name="lengths", bufs=LENGTHS))
         acc_psum = ctx.enter_context(tc.psum_pool(name="acc", bufs=1))
-        sum_psum = ctx.enter_context(tc.psum_pool(name="sums", bufs=1))
         ctx.enter_context(tc.manual_schedule())
 
         first_channel = keep.tile([P, TILES, COMPONENTS], BF16)
@@ -107,62 +121,80 @@ def tile_ryeelman_pa_t_kernel(
         nc.sync.dma_start(out=bias_rows[:], in_=b_ii.partition_broadcast(P))
         bias_column = keep.tile([P, 1], F32)
 
-        inv_codes = keep.tile([P, TILES, P], U32, align_bytes=64)
-        inv_planes = keep.tile([P, TILES, P], U8, align_bytes=64)
-        z_all = keep.tile([P, TILES, HIDDEN], F32)
+        lin_all = keep.tile([P, TILES, P], F32)
+        z_all = lin_all
 
         inv_tiles = {}
+        grouped_tiles = {}
         x_tiles = {}
-        square_tiles = {}
+        late_tiles = {}
+        early_tiles = {}
         factor_tiles = {}
+        xn_tiles = {}
         operand_tiles = {}
         product_tiles = {}
+        right_tiles = {}
         term_tiles = {}
         sum_tiles = {}
+        lin_tiles = {}
+        inv_operands = {}
 
         def bias_to_partitions():
             bias_f32 = keep.tile([P, HIDDEN], F32)
             nc.vector.tensor_copy(out=bias_f32[:], in_=bias_rows[:])
-            biasT = lengths_psum.tile([P, PACK, P], F32, tag="length2T")
+            biasT = lengths_psum.tile([P, PACK, P], F32, tag="small")
             nc.tensor.transpose(biasT[:, 0, :], bias_f32[:], identity[:])
             nc.vector.tensor_copy(out=bias_column[:], in_=biasT[:, 0, 0:1])
 
-        def load_invariants(chunk):
-            first = chunk * INV_CHUNK
-            inv_sb = inv_pool.tile([P, INV_CHUNK, FEATURES], BF16)
-            nc.sync.dma_start(out=inv_sb[:, :, 0:INPUT_FEATURES], in_=inv_input_rows[:, first : first + INV_CHUNK, :])
-            nc.sync.dma_start(
-                out=inv_sb[:, :, INPUT_FEATURES:FEATURES], in_=inv_hidden_rows[:, first : first + INV_CHUNK, :]
-            )
-            inv_tiles[chunk] = inv_sb
+        def load_invariants(c):
+            first = c * QUAD
+            inv_sb = inv_pool.tile([P, QUAD, FEATURES], BF16)
+            nc.sync.dma_start(out=inv_sb[:, :, 0:INPUT_FEATURES], in_=inv_input_rows[:, first : first + QUAD, :])
+            nc.sync.dma_start(out=inv_sb[:, :, INPUT_FEATURES:FEATURES], in_=inv_hidden_rows[:, first : first + QUAD, :])
+            inv_tiles[c] = inv_sb
 
-        grouped_tiles = {}
-
-        def group_invariants(chunk):
-            inv_sb = inv_tiles[chunk]
-            inv_grouped = inv_pool.tile([P, INV_CHUNK * P, PACK], BF16, align_bytes=64)
-            grouped_tiles[chunk] = inv_grouped
-            for pair in range(INV_CHUNK // 2):
+        def group_invariants(c):
+            inv_sb = inv_tiles[c]
+            inv_grouped = inv_pool.tile([P, QUAD * P, PACK], BF16, align_bytes=64)
+            grouped_tiles[c] = inv_grouped
+            for pair in range(QUAD // 2):
                 invT = words_psum.tile([P, 2, 2 * P], F32, tag="xT")
                 for i in range(2):
                     inv_words = inv_sb[:, 2 * pair + i, :].bitcast(F32)
                     for u in range(2):
-                        nc.tensor.transpose(
-                            invT[:, u, i * P : (i + 1) * P], inv_words[:, u : FEATURES // 2 : 2], identity[:]
-                        )
+                        nc.tensor.transpose(invT[:, u, i * P : (i + 1) * P], inv_words[:, u : FEATURES // 2 : 2], identity[:])
                 grouped_words = inv_grouped[:, 2 * pair * P : 2 * (pair + 1) * P, :].bitcast(F32)
-                if INV_ON_SCALAR:
-                    nc.scalar.copy(out=grouped_words, in_=invT[:].rearrange("p u c -> p c u"))
-                else:
-                    nc.vector.tensor_copy(out=grouped_words, in_=invT[:].rearrange("p u c -> p c u"))
+                nc.scalar.copy(out=grouped_words, in_=invT[:].rearrange("p u c -> p c u"))
 
-        def quantise_invariants(chunk):
-            first = chunk * INV_CHUNK
-            inv_grouped = grouped_tiles[chunk]
+        def quantise_invariants(c):
+            inv_codes = inv_pool.tile([P, QUAD * P], U32, align_bytes=64)
+            inv_planes = inv_pool.tile([P, QUAD * P], U8, align_bytes=64)
+            inv_operands[c] = (inv_codes, inv_planes)
             nc.vector.quantize_mx(
-                out=inv_codes[:, first : first + INV_CHUNK, :].rearrange("p i b -> p (i b)").bitcast(FP8X4),
-                scales=inv_planes[:, first : first + INV_CHUNK, :].rearrange("p i b -> p (i b)"),
-                in_=inv_grouped[:].rearrange("p c t -> p (c t)"),
+                out=inv_codes[:].bitcast(FP8X4),
+                scales=inv_planes[:],
+                in_=grouped_tiles[c][:].rearrange("p c t -> p (c t)"),
+            )
+
+        def linear_product(c):
+            inv_codes, inv_planes = inv_operands[c]
+            lin_ps = lengths_psum.tile([P, QUAD * P], F32, tag="small")
+            nc.tensor.matmul_mx(
+                out=lin_ps[:],
+                lhsT=w_codes[:, LINEAR, :].bitcast(FP8X4),
+                lhsT_scale=w_planes[:, LINEAR, :],
+                rhs=inv_codes[:].bitcast(FP8X4),
+                rhs_scale=inv_planes[:],
+                start=True,
+                stop=True,
+            )
+            lin_tiles[c] = lin_ps
+
+        def linear_out(c):
+            first = c * QUAD
+            nc.scalar.activation(
+                out=lin_all[:, first : first + QUAD, :].rearrange("p i b -> p (i b)"),
+                in_=lin_tiles[c][:], func=ACT.Identity, bias=bias_column[:], scale=1.0,
             )
 
         def load(t):
@@ -184,160 +216,170 @@ def tile_ryeelman_pa_t_kernel(
 
         def squares_on_gpsimd(t):
             stepped = stepped_halves(t)
-            late = work.tile([P, HALVES - SCALAR_HALVES, PACK, P], F32, bufs=4)
+            late = work.tile([P, HALVES - SCALAR_HALVES, PACK, P], F32, bufs=SQA + 4)
             for a in range(SCALAR_HALVES, GPSIMD_FIRST):
                 nc.vector.tensor_tensor(out=late[:, a - SCALAR_HALVES], in0=stepped[:, a], in1=stepped[:, a], op=ALU.mult)
             nc.vector.tensor_copy(out=x_tiles[t][:, :, 0:1], in_=first_channel[:, t, :].unsqueeze(2))
             for a in range(GPSIMD_FIRST, HALVES):
                 nc.gpsimd.tensor_tensor(out=late[:, a - SCALAR_HALVES], in0=stepped[:, a], in1=stepped[:, a], op=ALU.mult)
-            square_tiles[t] = [None, late]
+            late_tiles[t] = late
 
         def squares_on_scalar(t):
-            early = work.tile([P, SCALAR_HALVES, PACK, P], F32, bufs=3)
+            early = work.tile([P, SCALAR_HALVES, PACK, P], F32, bufs=4)
             nc.scalar.activation(out=early[:], in_=stepped_halves(t)[:, 0:SCALAR_HALVES], func=ACT.Square)
-            square_tiles[t][0] = early
+            early_tiles[t] = early
 
-        def inverse_lengths(t):
-            early, late = square_tiles[t]
-            inv_length = work.tile([P, PASSES, P, PACK], F32)
-            for g in range(PASSES):
-                length2T = lengths_psum.tile([P, PACK, P], F32, tag="length2T")
-                for k in range(PACK):
-                    for j in range(COMPONENTS):
-                        half = PASSES * j + g
-                        if half < SCALAR_HALVES:
-                            source = early[:, half, k, :]
-                        else:
-                            source = late[:, half - SCALAR_HALVES, k, :]
-                        nc.tensor.matmul(
-                            out=length2T[:, k, :],
-                            lhsT=source,
-                            rhs=identity[:],
-                            is_transpose=True,
-                            start=(j == 0),
-                            stop=(j == COMPONENTS - 1),
-                        )
-                nc.scalar.activation(
-                    out=inv_length[:, g],
-                    in_=length2T[:].rearrange("p k b -> p b k"),
-                    func=ACT.Abs_reciprocal_sqrt,
-                    bias=epsilon[:],
-                    scale=1.0,
-                )
-            factor_tiles[t] = inv_length
+        def inverse_lengths(t, g):
+            early, late = early_tiles[t], late_tiles[t]
+            if g == 0:
+                factor_tiles[t] = work.tile([P, PASSES, P, PACK], F32, name="inv_length")
+            inv_length = factor_tiles[t]
+            length2T = lengths_psum.tile([P, PACK, P], F32, tag="small")
+            for k in range(PACK):
+                for j in range(COMPONENTS):
+                    half = PASSES * j + g
+                    if half < SCALAR_HALVES:
+                        source = early[:, half, k, :]
+                    else:
+                        source = late[:, half - SCALAR_HALVES, k, :]
+                    nc.tensor.matmul(
+                        out=length2T[:, k, :],
+                        lhsT=source,
+                        rhs=identity[:],
+                        is_transpose=True,
+                        start=(j == 0),
+                        stop=(j == COMPONENTS - 1),
+                    )
+            nc.scalar.activation(
+                out=inv_length[:, g],
+                in_=length2T[:].rearrange("p k b -> p b k"),
+                func=ACT.Abs_reciprocal_sqrt,
+                bias=epsilon[:],
+                scale=1.0,
+            )
 
         def square_factor(t):
-            inv_length = factor_tiles[t]
-            factor = work.tile([P, PASSES, P, PACK], F32)
-            nc.scalar.activation(out=factor[:], in_=inv_length[:], func=ACT.Square)
+            factor = work.tile([P, PASSES, P, PACK], F32, bufs=3)
+            nc.scalar.activation(out=factor[:], in_=factor_tiles[t][:], func=ACT.Square)
             factor_tiles[t] = factor
 
-        def normalise_and_quantise(t):
+        def normalise(t, j):
             x_sb = x_tiles[t]
             factor = factor_tiles[t]
-            xn = work.tile([P, COMPONENTS, CHANNELS], BF16, align_bytes=64)
-            xn_codes = work.tile([P, COMPONENTS, PASSES * P], U32, align_bytes=64)
-            xn_planes = work.tile([P, COMPONENTS, PASSES * P], U8, align_bytes=64)
-            for j in range(COMPONENTS):
-                xT = words_psum.tile([P, 2, PASSES * P], F32, tag="xT")
-                x_words = x_sb[:, j, :].bitcast(F32)
-                for g in range(PASSES):
-                    for u in range(2):
-                        nc.tensor.transpose(
-                            xT[:, u, g * P : (g + 1) * P],
-                            x_words[:, g * 2 * P + u : (g + 1) * 2 * P : 2],
-                            identity[:],
-                        )
-                nc.vector.tensor_tensor(
-                    out=xn[:, j, :].rearrange("p (c u e) -> p c u e", u=2, e=2),
-                    in0=xT[:].bitcast(BF16).rearrange("p u (c e) -> p c u e", e=2),
-                    in1=factor[:].rearrange("p g b (u e) -> p (g b) u e", e=2),
-                    op=ALU.mult,
-                )
+            i = t % 2
+            if i == 0 and j == 0:
+                xn_tiles[t // 2] = work.tile([P, COMPONENTS, PASSES, 2, P * PACK], BF16, align_bytes=64, name="xn")
+            xn = xn_tiles[t // 2]
+            xT = words_psum.tile([P, 2, PASSES * P], F32, tag="xT")
+            x_words = x_sb[:, j, :].bitcast(F32)
+            for g in range(PASSES):
+                for u in range(2):
+                    nc.tensor.transpose(
+                        xT[:, u, g * P : (g + 1) * P],
+                        x_words[:, g * 2 * P + u : (g + 1) * 2 * P : 2],
+                        identity[:],
+                    )
+            nc.vector.tensor_tensor(
+                out=xn[:, j, :, i, :].rearrange("p g (b u e) -> p g b u e", u=2, e=2),
+                in0=xT[:].bitcast(BF16).rearrange("p u (g b e) -> p g b u e", g=PASSES, e=2),
+                in1=factor[:].rearrange("p g b (u e) -> p g b u e", e=2),
+                op=ALU.mult,
+            )
+
+        def quantise(p):
+            xn = xn_tiles[p]
+            xn_codes = work.tile([P, COMPONENTS, PASSES, 2 * P], U32, align_bytes=64)
+            xn_planes = work.tile([P, COMPONENTS, PASSES, 2 * P], U8, align_bytes=64)
             for first, last in ((0, 2), (2, 3)):
                 nc.vector.quantize_mx(
-                    out=xn_codes[:, first:last, :].rearrange("p j c -> p (j c)").bitcast(FP8X4),
-                    scales=xn_planes[:, first:last, :].rearrange("p j c -> p (j c)"),
-                    in_=xn[:, first:last, :].rearrange("p j c -> p (j c)"),
+                    out=xn_codes[:, first:last].rearrange("p j g c -> p (j g c)").bitcast(FP8X4),
+                    scales=xn_planes[:, first:last].rearrange("p j g c -> p (j g c)"),
+                    in_=xn[:, first:last].rearrange("p j g i c -> p (j g i c)"),
                 )
-            operand_tiles[t] = (xn_codes, xn_planes)
+            operand_tiles[p] = (xn_codes, xn_planes)
 
-        def multiply(t):
-            xn_codes, xn_planes = operand_tiles[t]
-            right_ps = acc_psum.tile([P, COMPONENTS + 1, P], F32, tag="right")
-            left_ps = acc_psum.tile([P, COMPONENTS + 1, P], F32, tag="left")
-            for side, acc in ((RIGHT, right_ps), (LEFT, left_ps)):
-                for j in range(COMPONENTS):
-                    for g in range(PASSES):
-                        nc.tensor.matmul_mx(
-                            out=acc[:, j, :],
-                            lhsT=w_codes[:, side + g, :].bitcast(FP8X4),
-                            lhsT_scale=w_planes[:, side + g, :],
-                            rhs=xn_codes[:, j, g * P : (g + 1) * P].bitcast(FP8X4),
-                            rhs_scale=xn_planes[:, j, g * P : (g + 1) * P],
-                            start=(g == 0),
-                            stop=(g == PASSES - 1),
-                        )
-                if side == RIGHT:
+        def multiply(p):
+            xn_codes, xn_planes = operand_tiles[p]
+            right01 = acc_psum.tile([P, 2, 2 * P], F32, tag="right01")
+            both2 = acc_psum.tile([P, 2, 2 * P], F32, tag="both2")
+            left01 = acc_psum.tile([P, 2, 2 * P], F32, tag="left01")
+            for side, j, acc, slot in (
+                (RIGHT, 0, right01, 0),
+                (RIGHT, 1, right01, 1),
+                (RIGHT, 2, both2, 0),
+                (LEFT, 2, both2, 1),
+                (LEFT, 0, left01, 0),
+                (LEFT, 1, left01, 1),
+            ):
+                for g in range(PASSES):
                     nc.tensor.matmul_mx(
-                        out=right_ps[:, COMPONENTS, :],
-                        lhsT=w_codes[:, LINEAR, :].bitcast(FP8X4),
-                        lhsT_scale=w_planes[:, LINEAR, :],
-                        rhs=inv_codes[:, t, :].bitcast(FP8X4),
-                        rhs_scale=inv_planes[:, t, :],
-                        start=True,
-                        stop=True,
+                        out=acc[:, slot, :],
+                        lhsT=w_codes[:, side + g, :].bitcast(FP8X4),
+                        lhsT_scale=w_planes[:, side + g, :],
+                        rhs=xn_codes[:, j, g, :].bitcast(FP8X4),
+                        rhs_scale=xn_planes[:, j, g, :],
+                        start=(g == 0),
+                        stop=(g == PASSES - 1),
                     )
-            product_tiles[t] = (left_ps, right_ps)
+            product_tiles[p] = (right01, both2, left01)
 
-        def combine(t):
-            left_ps, right_ps = product_tiles[t]
-            right_sb = work.tile([P, COMPONENTS, P], F32)
-            terms = work.tile([P, COMPONENTS + 1, P], F32)
-            nc.scalar.copy(out=right_sb[:], in_=right_ps[:, 0:COMPONENTS, :])
-            nc.scalar.activation(
-                out=terms[:, COMPONENTS, :], in_=right_ps[:, COMPONENTS, :], func=ACT.Identity, bias=bias_column[:], scale=1.0
+        def copies(p):
+            right01, both2, left01 = product_tiles[p]
+            right_sb = work.tile([P, COMPONENTS, 2 * P], F32)
+            nc.scalar.copy(out=right_sb[:, 0:2, :], in_=right01[:])
+            nc.scalar.copy(out=right_sb[:, 2, :], in_=both2[:, 0, :])
+            right_tiles[p] = right_sb
+
+        def combine(p):
+            right01, both2, left01 = product_tiles[p]
+            right_sb = right_tiles[p]
+            terms = work.tile([P, COMPONENTS, 2, P], F32)
+            nc.vector.tensor_tensor(
+                out=terms[:, 2].rearrange("p i b -> p (i b)"), in0=both2[:, 1, :], in1=right_sb[:, 2, :], op=ALU.mult
             )
             nc.vector.tensor_tensor(
-                out=terms[:, 0:COMPONENTS, :], in0=left_ps[:, 0:COMPONENTS, :], in1=right_sb[:], op=ALU.mult
+                out=terms[:, 0:2].rearrange("p j i b -> p j (i b)"), in0=left01[:], in1=right_sb[:, 0:2, :], op=ALU.mult
             )
-            term_tiles[t] = terms
+            term_tiles[p] = terms
 
-        def add_up(t):
-            if t % SUM_GROUP == 0:
-                sum_tiles[t // SUM_GROUP] = sum_psum.tile([P, SUM_GROUP, HIDDEN], F32, name="sums")
-            sums = sum_tiles[t // SUM_GROUP]
-            for s in range(COMPONENTS + 1):
-                nc.tensor.matmul(
-                    out=sums[:, t % SUM_GROUP, :],
-                    lhsT=term_tiles[t][:, s, :],
-                    rhs=identity[:],
-                    is_transpose=True,
-                    start=(s == 0),
-                    stop=(s == COMPONENTS),
-                )
+        def add_up(p):
+            terms = term_tiles[p]
+            sums = acc_psum.tile([P, 2, HIDDEN], F32, tag="right01")
+            for i in range(2):
+                sources = [lin_all[:, 2 * p + i, :]] + [terms[:, j, i, :] for j in range(COMPONENTS)]
+                for s in range(len(sources)):
+                    nc.tensor.matmul(
+                        out=sums[:, i, :],
+                        lhsT=sources[s],
+                        rhs=identity[:],
+                        is_transpose=True,
+                        start=(s == 0),
+                        stop=(s == COMPONENTS),
+                    )
+            sum_tiles[p] = sums
 
-        def collect(group):
-            nc.scalar.copy(out=z_all[:, group * SUM_GROUP : (group + 1) * SUM_GROUP, :], in_=sum_tiles[group][:])
+        def collect(p):
+            nc.scalar.copy(out=z_all[:, 2 * p : 2 * p + 2, :], in_=sum_tiles[p][:])
 
         def finish(begin, end):
             nc.scalar.activation(out=z_all[:, begin:end, :], in_=z_all[:, begin:end, :], func=ACT.Tanh)
             nc.sync.dma_start(out=out_rows[:, begin:end, :], in_=z_all[:, begin:end, :])
 
-        for t in range(LOAD_AHEAD - 1):
+        for t in range(LOAD_AHEAD):
             load(t)
-        for c in range(INV_CHUNKS):
-            if INV_L[c] == 0:
-                load_invariants(c)
-        load(LOAD_AHEAD - 1)
-        squares_on_gpsimd(0)
+            if INV_L[0] == 0 and t == 1:
+                load_invariants(0)
+        for t in range(SQA):
+            squares_on_gpsimd(t)
 
-        last_group = TILES // SUM_GROUP - 1
-        early_tiles = last_group * SUM_GROUP
-        for step in range(TILES + 6):
+        def at(step, lag):
+            q, r = divmod(step - lag, 2)
+            return q if r == 0 and 0 <= q < PAIRS else -1
+
+        for step in range(2 * (PAIRS - 1) + COS + 1):
             if step + LOAD_AHEAD < TILES:
                 load(step + LOAD_AHEAD)
-            for c in range(INV_CHUNKS):
+            for c in range(QUADS):
                 if INV_L[c] and step + 1 == INV_L[c]:
                     load_invariants(c)
             if step == 1:
@@ -345,40 +387,75 @@ def tile_ryeelman_pa_t_kernel(
                 load_weight(nc, w_codes, w_planes, LEFT, W_left_words, W_left_scales)
                 load_weight(nc, w_codes, w_planes, RIGHT, W_right_words, W_right_scales)
                 bias_to_partitions()
-            if SC_FIRST and step < TILES:
-                squares_on_scalar(step)
-            if 0 <= step - 2 < TILES:
-                inverse_lengths(step - 2)
+            p = at(step, COS)
+            if 0 <= p < PAIRS - 1 and not CO_MID:
+                collect(p)
+            p = at(step, CPS)
+            if p >= 0 and not CP_LATE:
+                copies(p)
+            p = at(step, MUS)
+            if p >= 0 and not CP_LATE and CB < 0:
+                combine(p)
+            pc = p
+            t = step - 2
+            if 0 <= t < TILES:
+                inverse_lengths(t, 0)
+                inverse_lengths(t, 1)
                 if not F_LATE:
-                    square_factor(step - 2)
-            if 0 <= step - 3 < TILES:
-                normalise_and_quantise(step - 3)
-            if step + 1 < TILES:
-                squares_on_gpsimd(step + 1)
-            for c in range(INV_CHUNKS):
-                if not INV_ON_SCALAR and step == INV_T[c]:
-                    group_invariants(c)
-            for c in range(INV_CHUNKS):
+                    square_factor(t)
+            p = at(step, ADS)
+            if p >= 0 and ADD_FIRST:
+                add_up(p)
+            t = step - 3
+            if 0 <= t < TILES:
+                for j in range(COMPONENTS):
+                    normalise(t, j)
+                    if pc >= 0 and CB == j:
+                        combine(pc)
+            elif pc >= 0 and CB >= 0:
+                combine(pc)
+            p = at(step, ADS)
+            if p >= 0 and not ADD_FIRST:
+                add_up(p)
+            p = at(step, QS)
+            if p >= 0:
+                quantise(p)
+            if step + SQA < TILES:
+                squares_on_gpsimd(step + SQA)
+            for c in range(QUADS):
                 if step == INV_Q[c]:
                     quantise_invariants(c)
-            if 0 <= step - 5 < TILES:
-                add_up(step - 5)
-            if 0 <= step - 4 < TILES:
-                multiply(step - 4)
-            if not SC_FIRST and step < TILES:
+            for c in range(QUADS):
+                if step == LIN[c]:
+                    linear_product(c)
+            p = at(step, MXS)
+            if p >= 0:
+                multiply(p)
+            if step < TILES:
                 squares_on_scalar(step)
-            if F_LATE and 0 <= step - 2 < TILES:
-                square_factor(step - 2)
-            for c in range(INV_CHUNKS):
-                if INV_ON_SCALAR and step == INV_T[c]:
+            p = at(step, COS)
+            if 0 <= p < PAIRS - 1 and CO_MID:
+                collect(p)
+            t = step - 2
+            if F_LATE and 0 <= t < TILES:
+                square_factor(t)
+            for c in range(QUADS):
+                if step == LIN[c]:
+                    linear_out(c)
+            for c in range(QUADS):
+                if step == INV_T[c]:
                     group_invariants(c)
-            if 0 <= step - 4 < TILES:
-                combine(step - 4)
-            if 0 <= step - 5 < early_tiles and (step - 5) % SUM_GROUP == SUM_GROUP - 1:
-                collect((step - 5) // SUM_GROUP)
+            p = at(step, CPS)
+            if p >= 0 and CP_LATE:
+                copies(p)
+            p = at(step, MUS)
+            if p >= 0 and CP_LATE:
+                combine(p)
+            piece = step - (TILES + 2)
             pieces = 3
-            piece = step - (TILES + 1)
+            ready = TILES - 8
             if 0 <= piece < pieces:
-                finish(early_tiles * piece // pieces, early_tiles * (piece + 1) // pieces)
-        nc.scalar.activation(out=z_all[:, early_tiles:TILES, :], in_=sum_tiles[last_group][:], func=ACT.Tanh)
-        nc.sync.dma_start(out=out_rows[:, early_tiles:TILES, :], in_=z_all[:, early_tiles:TILES, :])
+                finish(ready * piece // pieces, ready * (piece + 1) // pieces)
+        finish(TILES - 8, TILES - 2)
+        nc.scalar.activation(out=z_all[:, TILES - 2 :, :], in_=sum_tiles[PAIRS - 1][:], func=ACT.Tanh)
+        nc.sync.dma_start(out=out_rows[:, TILES - 2 :, :], in_=z_all[:, TILES - 2 :, :])

@@ -45,11 +45,20 @@ CP_LATE = False
 CO_MID = True
 SUMS_IN_ACC = True
 CB = -1
+ADD = ""
+V_FIRST = 1
+BIAS_DIRECT = True
+INV0_AFTER = 0
+DR_A = 12
+ADD_SLICES = PACK
+EPS_TILE = True
+VS = PACK
+G_MERGE = False
 LAST = 0
-INV_L = [0, 1, 2, 3, 4, 5, 6, 7]
-INV_T = [1, 3, 5, 7, 9, 11, 13, 15]
-INV_Q = [2, 4, 6, 8, 10, 12, 14, 16]
-LIN = [7, 9, 11, 13, 15, 17, 19, 21]
+INV_L = [0, 2, 6, 10, 14, 18, 22, 26]
+INV_T = [0, 5, 9, 13, 17, 21, 25, 29]
+INV_Q = [1, 6, 10, 14, 18, 22, 26, 30]
+LIN = [7, 9, 11, 15, 19, 23, 27, 31]
 F_LATE = False
 X_FIRST = False
 ADD_FIRST = False
@@ -117,9 +126,7 @@ def tile_ryeelman_pa_t_kernel(
         nc.scalar.activation(out=table_warmer[:], in_=epsilon[:], func=ACT.Abs_reciprocal_sqrt)
         identity = keep.tile([P, P], F32)
         make_identity(nc, identity[:])
-        bias_rows = keep.tile([P, HIDDEN], BF16)
-        nc.sync.dma_start(out=bias_rows[:], in_=b_ii.partition_broadcast(P))
-        bias_column = keep.tile([P, 1], F32)
+        bias_column = keep.tile([P, 1], BF16)
 
         lin_all = keep.tile([P, TILES, P], F32)
         z_all = lin_all
@@ -138,13 +145,6 @@ def tile_ryeelman_pa_t_kernel(
         sum_tiles = {}
         lin_tiles = {}
         inv_operands = {}
-
-        def bias_to_partitions():
-            bias_f32 = keep.tile([P, HIDDEN], F32)
-            nc.vector.tensor_copy(out=bias_f32[:], in_=bias_rows[:])
-            biasT = lengths_psum.tile([P, PACK, P], F32, tag="small")
-            nc.tensor.transpose(biasT[:, 0, :], bias_f32[:], identity[:])
-            nc.vector.tensor_copy(out=bias_column[:], in_=biasT[:, 0, 0:1])
 
         def load_invariants(c):
             first = c * QUAD
@@ -217,12 +217,30 @@ def tile_ryeelman_pa_t_kernel(
         def squares_on_gpsimd(t):
             stepped = stepped_halves(t)
             late = work.tile([P, HALVES - SCALAR_HALVES, PACK, P], F32, bufs=SQA + 4)
+            if ADD == "V" and t >= 1:
+                add_squares(nc.vector, t - 1)
             for a in range(SCALAR_HALVES, GPSIMD_FIRST):
-                nc.vector.tensor_tensor(out=late[:, a - SCALAR_HALVES], in0=stepped[:, a], in1=stepped[:, a], op=ALU.mult)
+                nc.vector.tensor_tensor(out=late[:, a - SCALAR_HALVES, 0:VS], in0=stepped[:, a, 0:VS], in1=stepped[:, a, 0:VS], op=ALU.mult)
             nc.vector.tensor_copy(out=x_tiles[t][:, :, 0:1], in_=first_channel[:, t, :].unsqueeze(2))
-            for a in range(GPSIMD_FIRST, HALVES):
-                nc.gpsimd.tensor_tensor(out=late[:, a - SCALAR_HALVES], in0=stepped[:, a], in1=stepped[:, a], op=ALU.mult)
+            if t < V_FIRST:
+                for a in range(GPSIMD_FIRST, HALVES):
+                    nc.vector.tensor_tensor(out=late[:, a - SCALAR_HALVES], in0=stepped[:, a], in1=stepped[:, a], op=ALU.mult)
+            elif G_MERGE:
+                nc.gpsimd.tensor_tensor(out=late[:, GPSIMD_FIRST - SCALAR_HALVES :], in0=stepped[:, GPSIMD_FIRST:], in1=stepped[:, GPSIMD_FIRST:], op=ALU.mult)
+            else:
+                for a in range(GPSIMD_FIRST, HALVES):
+                    nc.gpsimd.tensor_tensor(out=late[:, a - SCALAR_HALVES], in0=stepped[:, a], in1=stepped[:, a], op=ALU.mult)
+            if VS < PACK and SCALAR_HALVES < GPSIMD_FIRST:
+                a = SCALAR_HALVES
+                nc.gpsimd.tensor_tensor(out=late[:, 0, VS:], in0=stepped[:, a, VS:], in1=stepped[:, a, VS:], op=ALU.mult)
             late_tiles[t] = late
+            if ADD == "G":
+                add_squares(nc.gpsimd, t)
+
+        def add_squares(engine, t):
+            late = late_tiles[t]
+            a, b = 3 - SCALAR_HALVES, 5 - SCALAR_HALVES
+            engine.tensor_tensor(out=late[:, b, 0:ADD_SLICES], in0=late[:, a, 0:ADD_SLICES], in1=late[:, b, 0:ADD_SLICES], op=ALU.add)
 
         def squares_on_scalar(t):
             early = work.tile([P, SCALAR_HALVES, PACK, P], F32, bufs=4)
@@ -238,6 +256,8 @@ def tile_ryeelman_pa_t_kernel(
             for k in range(PACK):
                 for j in range(COMPONENTS):
                     half = PASSES * j + g
+                    if half == 3 and ADD and k < ADD_SLICES:
+                        continue
                     if half < SCALAR_HALVES:
                         source = early[:, half, k, :]
                     else:
@@ -254,7 +274,7 @@ def tile_ryeelman_pa_t_kernel(
                 out=inv_length[:, g],
                 in_=length2T[:].rearrange("p k b -> p b k"),
                 func=ACT.Abs_reciprocal_sqrt,
-                bias=epsilon[:],
+                bias=epsilon[:] if EPS_TILE else EPSILON,
                 scale=1.0,
             )
 
@@ -286,31 +306,41 @@ def tile_ryeelman_pa_t_kernel(
                 op=ALU.mult,
             )
 
-        def quantise(p):
+        def quantise(p, components):
             xn = xn_tiles[p]
-            xn_codes = work.tile([P, COMPONENTS, PASSES, 2 * P], U32, align_bytes=64)
-            xn_planes = work.tile([P, COMPONENTS, PASSES, 2 * P], U8, align_bytes=64)
-            for first, last in ((0, 2), (2, 3)):
+            if p not in operand_tiles:
+                xn_codes = work.tile([P, COMPONENTS, PASSES, 2 * P], U32, align_bytes=64)
+                xn_planes = work.tile([P, COMPONENTS, PASSES, 2 * P], U8, align_bytes=64)
+                operand_tiles[p] = (xn_codes, xn_planes)
+            xn_codes, xn_planes = operand_tiles[p]
+            for first, last in components:
                 nc.vector.quantize_mx(
                     out=xn_codes[:, first:last].rearrange("p j g c -> p (j g c)").bitcast(FP8X4),
                     scales=xn_planes[:, first:last].rearrange("p j g c -> p (j g c)"),
                     in_=xn[:, first:last].rearrange("p j g i c -> p (j g i c)"),
                 )
-            operand_tiles[p] = (xn_codes, xn_planes)
 
         def multiply(p):
             xn_codes, xn_planes = operand_tiles[p]
-            right01 = acc_psum.tile([P, 2, 2 * P], F32, tag="right01")
-            both2 = acc_psum.tile([P, 2, 2 * P], F32, tag="both2")
-            left01 = acc_psum.tile([P, 2, 2 * P], F32, tag="left01")
-            for side, j, acc, slot in (
+            if p < PAIRS - 1:
+                right01 = acc_psum.tile([P, 2, 2 * P], F32, tag="right01")
+                both2 = acc_psum.tile([P, 2, 2 * P], F32, tag="both2")
+                left01 = acc_psum.tile([P, 2, 2 * P], F32, tag="left01")
+            else:
+                right01 = words_psum.tile([P, 2, 2 * P], F32, tag="xT")
+                left01 = words_psum.tile([P, 2, 2 * P], F32, tag="xT")
+                both2 = words_psum.tile([P, 2, 2 * P], F32, tag="xT")
+            order = [
                 (RIGHT, 0, right01, 0),
                 (RIGHT, 1, right01, 1),
                 (RIGHT, 2, both2, 0),
                 (LEFT, 2, both2, 1),
                 (LEFT, 0, left01, 0),
                 (LEFT, 1, left01, 1),
-            ):
+            ]
+            if p == PAIRS - 1:
+                order = [order[i] for i in (0, 4, 1, 5, 2, 3)]
+            for side, j, acc, slot in order:
                 for g in range(PASSES):
                     nc.tensor.matmul_mx(
                         out=acc[:, slot, :],
@@ -334,17 +364,25 @@ def tile_ryeelman_pa_t_kernel(
             right01, both2, left01 = product_tiles[p]
             right_sb = right_tiles[p]
             terms = work.tile([P, COMPONENTS, 2, P], F32)
-            nc.vector.tensor_tensor(
-                out=terms[:, 2].rearrange("p i b -> p (i b)"), in0=both2[:, 1, :], in1=right_sb[:, 2, :], op=ALU.mult
-            )
+            def third():
+                nc.vector.tensor_tensor(
+                    out=terms[:, 2].rearrange("p i b -> p (i b)"), in0=both2[:, 1, :], in1=right_sb[:, 2, :], op=ALU.mult
+                )
+            if p < PAIRS - 1:
+                third()
             nc.vector.tensor_tensor(
                 out=terms[:, 0:2].rearrange("p j i b -> p j (i b)"), in0=left01[:], in1=right_sb[:, 0:2, :], op=ALU.mult
             )
+            if p == PAIRS - 1:
+                third()
             term_tiles[p] = terms
 
         def add_up(p):
             terms = term_tiles[p]
-            sums = acc_psum.tile([P, 2, HIDDEN], F32, tag="right01")
+            if p < PAIRS - 4:
+                sums = acc_psum.tile([P, 2, HIDDEN], F32, tag="right01")
+            else:
+                sums = lengths_psum.tile([P, 2, HIDDEN], F32, tag="small")
             for i in range(2):
                 sources = [lin_all[:, 2 * p + i, :]] + [terms[:, j, i, :] for j in range(COMPONENTS)]
                 for s in range(len(sources)):
@@ -359,7 +397,10 @@ def tile_ryeelman_pa_t_kernel(
             sum_tiles[p] = sums
 
         def collect(p):
-            nc.scalar.copy(out=z_all[:, 2 * p : 2 * p + 2, :], in_=sum_tiles[p][:])
+            if p < PAIRS - 4:
+                nc.scalar.copy(out=z_all[:, 2 * p : 2 * p + 2, :], in_=sum_tiles[p][:])
+            else:
+                nc.scalar.activation(out=z_all[:, 2 * p : 2 * p + 2, :], in_=sum_tiles[p][:], func=ACT.Tanh)
 
         def finish(begin, end):
             nc.scalar.activation(out=z_all[:, begin:end, :], in_=z_all[:, begin:end, :], func=ACT.Tanh)
@@ -367,7 +408,7 @@ def tile_ryeelman_pa_t_kernel(
 
         for t in range(LOAD_AHEAD):
             load(t)
-            if INV_L[0] == 0 and t == 1:
+            if INV_L[0] == 0 and t == INV0_AFTER:
                 load_invariants(0)
         for t in range(SQA):
             squares_on_gpsimd(t)
@@ -376,7 +417,7 @@ def tile_ryeelman_pa_t_kernel(
             q, r = divmod(step - lag, 2)
             return q if r == 0 and 0 <= q < PAIRS else -1
 
-        for step in range(2 * (PAIRS - 1) + COS + 1):
+        for step in range(TILES + 2):
             if step + LOAD_AHEAD < TILES:
                 load(step + LOAD_AHEAD)
             for c in range(QUADS):
@@ -386,7 +427,7 @@ def tile_ryeelman_pa_t_kernel(
                 load_weight(nc, w_codes, w_planes, LINEAR, W_ii_words, W_ii_scales)
                 load_weight(nc, w_codes, w_planes, LEFT, W_left_words, W_left_scales)
                 load_weight(nc, w_codes, w_planes, RIGHT, W_right_words, W_right_scales)
-                bias_to_partitions()
+                nc.sync.dma_start(out=bias_column[:], in_=b_ii.rearrange("(h o) -> h o", o=1))
             p = at(step, COS)
             if 0 <= p < PAIRS - 1 and not CO_MID:
                 collect(p)
@@ -419,9 +460,11 @@ def tile_ryeelman_pa_t_kernel(
                 add_up(p)
             p = at(step, QS)
             if p >= 0:
-                quantise(p)
+                quantise(p, ((0, 2), (2, 3)))
             if step + SQA < TILES:
                 squares_on_gpsimd(step + SQA)
+            elif ADD == "V" and step + SQA == TILES:
+                add_squares(nc.vector, TILES - 1)
             for c in range(QUADS):
                 if step == INV_Q[c]:
                     quantise_invariants(c)
@@ -451,11 +494,29 @@ def tile_ryeelman_pa_t_kernel(
             p = at(step, MUS)
             if p >= 0 and CP_LATE:
                 combine(p)
-            piece = step - (TILES + 2)
-            pieces = 3
-            ready = TILES - 8
-            if 0 <= piece < pieces:
-                finish(ready * piece // pieces, ready * (piece + 1) // pieces)
-        finish(TILES - 8, TILES - 2)
-        nc.scalar.activation(out=z_all[:, TILES - 2 :, :], in_=sum_tiles[PAIRS - 1][:], func=ACT.Tanh)
+
+        copies(PAIRS - 3)
+        combine(PAIRS - 3)
+        normalise(TILES - 1, 0)
+        normalise(TILES - 1, 1)
+        quantise(PAIRS - 1, ((0, 1),))
+        normalise(TILES - 1, 2)
+        add_up(PAIRS - 4)
+        multiply(PAIRS - 2)
+        collect(PAIRS - 4)
+        finish(0, DR_A)
+        copies(PAIRS - 2)
+        quantise(PAIRS - 1, ((1, 2), (2, 3)))
+        combine(PAIRS - 2)
+        add_up(PAIRS - 3)
+        multiply(PAIRS - 1)
+        collect(PAIRS - 3)
+        finish(DR_A, TILES - 8)
+        add_up(PAIRS - 2)
+        copies(PAIRS - 1)
+        collect(PAIRS - 2)
+        nc.sync.dma_start(out=out_rows[:, TILES - 8 : TILES - 2, :], in_=z_all[:, TILES - 8 : TILES - 2, :])
+        combine(PAIRS - 1)
+        add_up(PAIRS - 1)
+        collect(PAIRS - 1)
         nc.sync.dma_start(out=out_rows[:, TILES - 2 :, :], in_=z_all[:, TILES - 2 :, :])

@@ -46,20 +46,28 @@ CO_MID = True
 SUMS_IN_ACC = True
 CB = -1
 ADD = ""
-V_FIRST = 1
+S_ZERO = 3
+HEAD = 0
+HEAD_S = 2
+HEAD_V = 2
+MIN_S = 2
+INV0_V = False
+XT0 = False
 BIAS_DIRECT = True
 INV0_AFTER = 0
 DR_A = 12
 ADD_SLICES = PACK
 EPS_TILE = True
+VE = 0
+VO = 0
 VS = PACK
-G_MERGE = False
+G_MERGE = True
 LAST = 0
 INV_L = [0, 2, 6, 10, 14, 18, 22, 26]
 INV_T = [0, 5, 9, 13, 17, 21, 25, 29]
 INV_Q = [1, 6, 10, 14, 18, 22, 26, 30]
 LIN = [7, 9, 11, 15, 19, 23, 27, 31]
-F_LATE = False
+F_LATE = True
 X_FIRST = False
 ADD_FIRST = False
 
@@ -138,6 +146,7 @@ def tile_ryeelman_pa_t_kernel(
         early_tiles = {}
         factor_tiles = {}
         xn_tiles = {}
+        xT_tiles = {}
         operand_tiles = {}
         product_tiles = {}
         right_tiles = {}
@@ -164,7 +173,10 @@ def tile_ryeelman_pa_t_kernel(
                     for u in range(2):
                         nc.tensor.transpose(invT[:, u, i * P : (i + 1) * P], inv_words[:, u : FEATURES // 2 : 2], identity[:])
                 grouped_words = inv_grouped[:, 2 * pair * P : 2 * (pair + 1) * P, :].bitcast(F32)
-                nc.scalar.copy(out=grouped_words, in_=invT[:].rearrange("p u c -> p c u"))
+                if INV0_V and c == 0:
+                    nc.vector.tensor_copy(out=grouped_words, in_=invT[:].rearrange("p u c -> p c u"))
+                else:
+                    nc.scalar.copy(out=grouped_words, in_=invT[:].rearrange("p u c -> p c u"))
 
         def quantise_invariants(c):
             inv_codes = inv_pool.tile([P, QUAD * P], U32, align_bytes=64)
@@ -214,37 +226,46 @@ def tile_ryeelman_pa_t_kernel(
             halves = x_tiles[t][:].rearrange("p j (g c) -> p (j g) c", g=PASSES)
             return halves.rearrange("p a (q k) -> p a k q", k=PACK)
 
+        def split(t):
+            if t == 0:
+                return S_ZERO, HALVES - S_ZERO
+            if t < HEAD:
+                return HEAD_S, HEAD_V
+            return SCALAR_HALVES, VE if t % 2 == 0 else VO
+
         def squares_on_gpsimd(t):
             stepped = stepped_halves(t)
-            late = work.tile([P, HALVES - SCALAR_HALVES, PACK, P], F32, bufs=SQA + 4)
-            if ADD == "V" and t >= 1:
-                add_squares(nc.vector, t - 1)
-            for a in range(SCALAR_HALVES, GPSIMD_FIRST):
-                nc.vector.tensor_tensor(out=late[:, a - SCALAR_HALVES, 0:VS], in0=stepped[:, a, 0:VS], in1=stepped[:, a, 0:VS], op=ALU.mult)
-            nc.vector.tensor_copy(out=x_tiles[t][:, :, 0:1], in_=first_channel[:, t, :].unsqueeze(2))
-            if t < V_FIRST:
-                for a in range(GPSIMD_FIRST, HALVES):
-                    nc.vector.tensor_tensor(out=late[:, a - SCALAR_HALVES], in0=stepped[:, a], in1=stepped[:, a], op=ALU.mult)
-            elif G_MERGE:
-                nc.gpsimd.tensor_tensor(out=late[:, GPSIMD_FIRST - SCALAR_HALVES :], in0=stepped[:, GPSIMD_FIRST:], in1=stepped[:, GPSIMD_FIRST:], op=ALU.mult)
-            else:
-                for a in range(GPSIMD_FIRST, HALVES):
-                    nc.gpsimd.tensor_tensor(out=late[:, a - SCALAR_HALVES], in0=stepped[:, a], in1=stepped[:, a], op=ALU.mult)
-            if VS < PACK and SCALAR_HALVES < GPSIMD_FIRST:
-                a = SCALAR_HALVES
-                nc.gpsimd.tensor_tensor(out=late[:, 0, VS:], in0=stepped[:, a, VS:], in1=stepped[:, a, VS:], op=ALU.mult)
+            late = work.tile([P, HALVES - MIN_S, PACK, P], F32, bufs=SQA + 4)
+            s, v = split(t)
+            early_head = t == 0 or t < HEAD
+            if early_head:
+                nc.vector.tensor_copy(out=x_tiles[t][:, :, 0:1], in_=first_channel[:, t, :].unsqueeze(2))
+            for a in range(s, s + v):
+                vs = PACK if early_head else VS
+                nc.vector.tensor_tensor(out=late[:, a - MIN_S, 0:vs], in0=stepped[:, a, 0:vs], in1=stepped[:, a, 0:vs], op=ALU.mult)
+            if not early_head:
+                nc.vector.tensor_copy(out=x_tiles[t][:, :, 0:1], in_=first_channel[:, t, :].unsqueeze(2))
+            if G_MERGE and s + v < HALVES:
+                nc.gpsimd.tensor_tensor(out=late[:, s + v - MIN_S :], in0=stepped[:, s + v :], in1=stepped[:, s + v :], op=ALU.mult)
+            elif not G_MERGE:
+                for a in range(s + v, HALVES):
+                    nc.gpsimd.tensor_tensor(out=late[:, a - MIN_S], in0=stepped[:, a], in1=stepped[:, a], op=ALU.mult)
+            if VS < PACK and v and not early_head:
+                a = s
+                nc.gpsimd.tensor_tensor(out=late[:, a - MIN_S, VS:], in0=stepped[:, a, VS:], in1=stepped[:, a, VS:], op=ALU.mult)
             late_tiles[t] = late
             if ADD == "G":
                 add_squares(nc.gpsimd, t)
 
         def add_squares(engine, t):
             late = late_tiles[t]
-            a, b = 3 - SCALAR_HALVES, 5 - SCALAR_HALVES
+            a, b = 3 - MIN_S, 5 - MIN_S
             engine.tensor_tensor(out=late[:, b, 0:ADD_SLICES], in0=late[:, a, 0:ADD_SLICES], in1=late[:, b, 0:ADD_SLICES], op=ALU.add)
 
         def squares_on_scalar(t):
+            s = split(t)[0]
             early = work.tile([P, SCALAR_HALVES, PACK, P], F32, bufs=4)
-            nc.scalar.activation(out=early[:], in_=stepped_halves(t)[:, 0:SCALAR_HALVES], func=ACT.Square)
+            nc.scalar.activation(out=early[:, 0:s], in_=stepped_halves(t)[:, 0:s], func=ACT.Square)
             early_tiles[t] = early
 
         def inverse_lengths(t, g):
@@ -258,10 +279,10 @@ def tile_ryeelman_pa_t_kernel(
                     half = PASSES * j + g
                     if half == 3 and ADD and k < ADD_SLICES:
                         continue
-                    if half < SCALAR_HALVES:
+                    if half < split(t)[0]:
                         source = early[:, half, k, :]
                     else:
-                        source = late[:, half - SCALAR_HALVES, k, :]
+                        source = late[:, half - MIN_S, k, :]
                     nc.tensor.matmul(
                         out=length2T[:, k, :],
                         lhsT=source,
@@ -283,14 +304,10 @@ def tile_ryeelman_pa_t_kernel(
             nc.scalar.activation(out=factor[:], in_=factor_tiles[t][:], func=ACT.Square)
             factor_tiles[t] = factor
 
-        def normalise(t, j):
+        def transpose_words(t, j):
             x_sb = x_tiles[t]
-            factor = factor_tiles[t]
-            i = t % 2
-            if i == 0 and j == 0:
-                xn_tiles[t // 2] = work.tile([P, COMPONENTS, PASSES, 2, P * PACK], BF16, align_bytes=64, name="xn")
-            xn = xn_tiles[t // 2]
             xT = words_psum.tile([P, 2, PASSES * P], F32, tag="xT")
+            xT_tiles[t, j] = xT
             x_words = x_sb[:, j, :].bitcast(F32)
             for g in range(PASSES):
                 for u in range(2):
@@ -299,6 +316,16 @@ def tile_ryeelman_pa_t_kernel(
                         x_words[:, g * 2 * P + u : (g + 1) * 2 * P : 2],
                         identity[:],
                     )
+
+        def normalise(t, j):
+            factor = factor_tiles[t]
+            i = t % 2
+            if i == 0 and j == 0:
+                xn_tiles[t // 2] = work.tile([P, COMPONENTS, PASSES, 2, P * PACK], BF16, align_bytes=64, name="xn")
+            xn = xn_tiles[t // 2]
+            if (t, j) not in xT_tiles:
+                transpose_words(t, j)
+            xT = xT_tiles[t, j]
             nc.vector.tensor_tensor(
                 out=xn[:, j, :, i, :].rearrange("p g (b u e) -> p g b u e", u=2, e=2),
                 in0=xT[:].bitcast(BF16).rearrange("p u (g b e) -> p g b u e", g=PASSES, e=2),
@@ -412,6 +439,9 @@ def tile_ryeelman_pa_t_kernel(
                 load_invariants(0)
         for t in range(SQA):
             squares_on_gpsimd(t)
+        if XT0:
+            for j in range(COMPONENTS):
+                transpose_words(0, j)
 
         def at(step, lag):
             q, r = divmod(step - lag, 2)

@@ -44,20 +44,20 @@ COS = 10
 CP_LATE = False
 CO_MID = True
 SUMS_IN_ACC = True
-CB = -1
 ADD = ""
 S_ZERO = 3
 HEAD = 0
 HEAD_S = 2
 HEAD_V = 2
 MIN_S = 2
-INV0_V = False
-XT0 = False
+INV_VEC = ()
+COL_V = True
+LIN_V = False
 BIAS_DIRECT = True
 INV0_AFTER = 0
 DR_A = 12
 ADD_SLICES = PACK
-EPS_TILE = True
+EPS_TILE = False
 VE = 0
 VO = 0
 VS = PACK
@@ -68,8 +68,13 @@ INV_T = [0, 5, 9, 13, 17, 21, 25, 29]
 INV_Q = [1, 6, 10, 14, 18, 22, 26, 30]
 LIN = [7, 9, 11, 15, 19, 23, 27, 31]
 F_LATE = True
-X_FIRST = False
-ADD_FIRST = False
+ORDER = [("s", 0, 4), ("r", 0, 0), ("s", 10, 4), ("r", 1, 0), ("x", 0, 0), ("x", 1, 0), ("x", 2, 0)]
+SQ_AFTER = -1
+WARM0 = 0
+WARM_STEPS = {}
+WARM_MX = {}
+W_AT = 1
+XL = 3
 
 LEFT, RIGHT, LINEAR = 0, 2, 4
 WEIGHT_SLOTS = 5
@@ -114,7 +119,7 @@ def tile_ryeelman_pa_t_kernel(
     with ExitStack() as ctx:
         keep = ctx.enter_context(tc.tile_pool(name="keep", bufs=1))
         inv_pool = ctx.enter_context(tc.tile_pool(name="inv", bufs=3))
-        x_pool = ctx.enter_context(tc.tile_pool(name="x", bufs=LOAD_AHEAD + 4))
+        x_pool = ctx.enter_context(tc.tile_pool(name="x", bufs=LOAD_AHEAD + XL + 1))
         work = ctx.enter_context(tc.tile_pool(name="work", bufs=2))
         words_psum = ctx.enter_context(tc.psum_pool(name="words", bufs=WORDS))
         lengths_psum = ctx.enter_context(tc.psum_pool(name="lengths", bufs=LENGTHS))
@@ -139,6 +144,8 @@ def tile_ryeelman_pa_t_kernel(
         lin_all = keep.tile([P, TILES, P], F32)
         z_all = lin_all
 
+        warm_sb = keep.tile([P, 4 * P], BF16)
+        nc.vector.memset(warm_sb[:], 1.0)
         inv_tiles = {}
         grouped_tiles = {}
         x_tiles = {}
@@ -147,6 +154,7 @@ def tile_ryeelman_pa_t_kernel(
         factor_tiles = {}
         xn_tiles = {}
         xT_tiles = {}
+        length_tiles = {}
         operand_tiles = {}
         product_tiles = {}
         right_tiles = {}
@@ -173,7 +181,7 @@ def tile_ryeelman_pa_t_kernel(
                     for u in range(2):
                         nc.tensor.transpose(invT[:, u, i * P : (i + 1) * P], inv_words[:, u : FEATURES // 2 : 2], identity[:])
                 grouped_words = inv_grouped[:, 2 * pair * P : 2 * (pair + 1) * P, :].bitcast(F32)
-                if INV0_V and c == 0:
+                if c in INV_VEC:
                     nc.vector.tensor_copy(out=grouped_words, in_=invT[:].rearrange("p u c -> p c u"))
                 else:
                     nc.scalar.copy(out=grouped_words, in_=invT[:].rearrange("p u c -> p c u"))
@@ -204,10 +212,15 @@ def tile_ryeelman_pa_t_kernel(
 
         def linear_out(c):
             first = c * QUAD
-            nc.scalar.activation(
-                out=lin_all[:, first : first + QUAD, :].rearrange("p i b -> p (i b)"),
-                in_=lin_tiles[c][:], func=ACT.Identity, bias=bias_column[:], scale=1.0,
-            )
+            if LIN_V:
+                nc.vector.tensor_scalar(
+                    out=lin_all[:, first : first + QUAD, :].rearrange("p i b -> p (i b)"), in0=lin_tiles[c][:], scalar1=bias_column[:], scalar2=None, op0=ALU.add,
+                )
+            else:
+                nc.scalar.activation(
+                    out=lin_all[:, first : first + QUAD, :].rearrange("p i b -> p (i b)"),
+                    in_=lin_tiles[c][:], func=ACT.Identity, bias=bias_column[:], scale=1.0,
+                )
 
         def load(t):
             x_sb = x_pool.tile([P, COMPONENTS, CHANNELS], BF16)
@@ -268,54 +281,58 @@ def tile_ryeelman_pa_t_kernel(
             nc.scalar.activation(out=early[:, 0:s], in_=stepped_halves(t)[:, 0:s], func=ACT.Square)
             early_tiles[t] = early
 
-        def inverse_lengths(t, g):
+        def open_lengths(t):
+            factor_tiles[t] = work.tile([P, PASSES, P, PACK], F32, name="inv_length")
+
+        def sum_squares(t, g, k):
             early, late = early_tiles[t], late_tiles[t]
-            if g == 0:
-                factor_tiles[t] = work.tile([P, PASSES, P, PACK], F32, name="inv_length")
-            inv_length = factor_tiles[t]
-            length2T = lengths_psum.tile([P, PACK, P], F32, tag="small")
-            for k in range(PACK):
-                for j in range(COMPONENTS):
-                    half = PASSES * j + g
-                    if half == 3 and ADD and k < ADD_SLICES:
-                        continue
-                    if half < split(t)[0]:
-                        source = early[:, half, k, :]
-                    else:
-                        source = late[:, half - MIN_S, k, :]
-                    nc.tensor.matmul(
-                        out=length2T[:, k, :],
-                        lhsT=source,
-                        rhs=identity[:],
-                        is_transpose=True,
-                        start=(j == 0),
-                        stop=(j == COMPONENTS - 1),
-                    )
+            if k == 0:
+                length_tiles[t, g] = lengths_psum.tile([P, PACK, P], F32, name="length2T", tag="small")
+            for j in range(COMPONENTS):
+                half = PASSES * j + g
+                if half == 3 and ADD and k < ADD_SLICES:
+                    continue
+                if half < split(t)[0]:
+                    source = early[:, half, k, :]
+                else:
+                    source = late[:, half - MIN_S, k, :]
+                nc.tensor.matmul(
+                    out=length_tiles[t, g][:, k, :],
+                    lhsT=source,
+                    rhs=identity[:],
+                    is_transpose=True,
+                    start=(j == 0),
+                    stop=(j == COMPONENTS - 1),
+                )
+
+        def inverse_lengths(t, g):
             nc.scalar.activation(
-                out=inv_length[:, g],
-                in_=length2T[:].rearrange("p k b -> p b k"),
+                out=factor_tiles[t][:, g],
+                in_=length_tiles[t, g][:].rearrange("p k b -> p b k"),
                 func=ACT.Abs_reciprocal_sqrt,
                 bias=epsilon[:] if EPS_TILE else EPSILON,
                 scale=1.0,
             )
 
         def square_factor(t):
-            factor = work.tile([P, PASSES, P, PACK], F32, bufs=3)
+            factor = work.tile([P, PASSES, P, PACK], F32, bufs=XL)
             nc.scalar.activation(out=factor[:], in_=factor_tiles[t][:], func=ACT.Square)
             factor_tiles[t] = factor
 
+        def transpose_word(t, j, g, u):
+            if g == 0 and u == 0:
+                xT_tiles[t, j] = words_psum.tile([P, 2, PASSES * P], F32, tag="xT", name="xT")
+            x_words = x_tiles[t][:, j, :].bitcast(F32)
+            nc.tensor.transpose(
+                xT_tiles[t, j][:, u, g * P : (g + 1) * P],
+                x_words[:, g * 2 * P + u : (g + 1) * 2 * P : 2],
+                identity[:],
+            )
+
         def transpose_words(t, j):
-            x_sb = x_tiles[t]
-            xT = words_psum.tile([P, 2, PASSES * P], F32, tag="xT")
-            xT_tiles[t, j] = xT
-            x_words = x_sb[:, j, :].bitcast(F32)
             for g in range(PASSES):
                 for u in range(2):
-                    nc.tensor.transpose(
-                        xT[:, u, g * P : (g + 1) * P],
-                        x_words[:, g * 2 * P + u : (g + 1) * 2 * P : 2],
-                        identity[:],
-                    )
+                    transpose_word(t, j, g, u)
 
         def normalise(t, j):
             factor = factor_tiles[t]
@@ -323,8 +340,6 @@ def tile_ryeelman_pa_t_kernel(
             if i == 0 and j == 0:
                 xn_tiles[t // 2] = work.tile([P, COMPONENTS, PASSES, 2, P * PACK], BF16, align_bytes=64, name="xn")
             xn = xn_tiles[t // 2]
-            if (t, j) not in xT_tiles:
-                transpose_words(t, j)
             xT = xT_tiles[t, j]
             nc.vector.tensor_tensor(
                 out=xn[:, j, :, i, :].rearrange("p g (b u e) -> p g b u e", u=2, e=2),
@@ -332,6 +347,37 @@ def tile_ryeelman_pa_t_kernel(
                 in1=factor[:].rearrange("p g b (u e) -> p g b u e", e=2),
                 op=ALU.mult,
             )
+
+        def keep_clock(n):
+            warm_ps = lengths_psum.tile([P, 4 * P], F32, tag="small")
+            for i in range(n):
+                nc.tensor.matmul(out=warm_ps[:], lhsT=warm_sb[:, 0:P], rhs=warm_sb[:], start=True, stop=True)
+
+        def keep_clock_mx(n):
+            warm_ps = lengths_psum.tile([P, 4 * P], F32, tag="small")
+            inv_codes, inv_planes = inv_operands[0]
+            for i in range(n):
+                nc.tensor.matmul_mx(out=warm_ps[:], lhsT=w_codes[:, LINEAR, :].bitcast(FP8X4), lhsT_scale=w_planes[:, LINEAR, :], rhs=inv_codes[:].bitcast(FP8X4), rhs_scale=inv_planes[:], start=True, stop=True)
+
+        def transposes(ts, tx, new):
+            sums = 0 <= ts < TILES
+            words = 0 <= tx < TILES
+            if sums:
+                open_lengths(ts)
+            for kind, a, b in ORDER:
+                if kind == "s" and sums:
+                    for k in range(a % 10, b):
+                        sum_squares(ts, a // 10, k)
+                if kind == "r":
+                    if sums:
+                        inverse_lengths(ts, a)
+                    if a == SQ_AFTER and new < TILES:
+                        squares_on_scalar(new)
+                if kind == "x" and words:
+                    transpose_words(tx, a)
+                    normalise(tx, a)
+                if kind == "f" and sums:
+                    square_factor(ts)
 
         def quantise(p, components):
             xn = xn_tiles[p]
@@ -425,7 +471,10 @@ def tile_ryeelman_pa_t_kernel(
 
         def collect(p):
             if p < PAIRS - 4:
-                nc.scalar.copy(out=z_all[:, 2 * p : 2 * p + 2, :], in_=sum_tiles[p][:])
+                if COL_V:
+                    nc.vector.tensor_copy(out=z_all[:, 2 * p : 2 * p + 2, :], in_=sum_tiles[p][:])
+                else:
+                    nc.scalar.copy(out=z_all[:, 2 * p : 2 * p + 2, :], in_=sum_tiles[p][:])
             else:
                 nc.scalar.activation(out=z_all[:, 2 * p : 2 * p + 2, :], in_=sum_tiles[p][:], func=ACT.Tanh)
 
@@ -439,21 +488,24 @@ def tile_ryeelman_pa_t_kernel(
                 load_invariants(0)
         for t in range(SQA):
             squares_on_gpsimd(t)
-        if XT0:
-            for j in range(COMPONENTS):
-                transpose_words(0, j)
 
         def at(step, lag):
-            q, r = divmod(step - lag, 2)
+            q, r = divmod(step - lag - XL + 3, 2)
             return q if r == 0 and 0 <= q < PAIRS else -1
 
-        for step in range(TILES + 2):
+        if WARM0:
+            keep_clock(WARM0)
+        for step in range(TILES + XL - 1):
+            if WARM_STEPS.get(step, 0):
+                keep_clock(WARM_STEPS[step])
+            if WARM_MX.get(step, 0):
+                keep_clock_mx(WARM_MX[step])
             if step + LOAD_AHEAD < TILES:
                 load(step + LOAD_AHEAD)
             for c in range(QUADS):
                 if INV_L[c] and step + 1 == INV_L[c]:
                     load_invariants(c)
-            if step == 1:
+            if step == W_AT:
                 load_weight(nc, w_codes, w_planes, LINEAR, W_ii_words, W_ii_scales)
                 load_weight(nc, w_codes, w_planes, LEFT, W_left_words, W_left_scales)
                 load_weight(nc, w_codes, w_planes, RIGHT, W_right_words, W_right_scales)
@@ -465,28 +517,11 @@ def tile_ryeelman_pa_t_kernel(
             if p >= 0 and not CP_LATE:
                 copies(p)
             p = at(step, MUS)
-            if p >= 0 and not CP_LATE and CB < 0:
+            if p >= 0 and not CP_LATE:
                 combine(p)
-            pc = p
-            t = step - 2
-            if 0 <= t < TILES:
-                inverse_lengths(t, 0)
-                inverse_lengths(t, 1)
-                if not F_LATE:
-                    square_factor(t)
+            transposes(step - 2, step - XL, step)
             p = at(step, ADS)
-            if p >= 0 and ADD_FIRST:
-                add_up(p)
-            t = step - 3
-            if 0 <= t < TILES:
-                for j in range(COMPONENTS):
-                    normalise(t, j)
-                    if pc >= 0 and CB == j:
-                        combine(pc)
-            elif pc >= 0 and CB >= 0:
-                combine(pc)
-            p = at(step, ADS)
-            if p >= 0 and not ADD_FIRST:
+            if p >= 0:
                 add_up(p)
             p = at(step, QS)
             if p >= 0:
@@ -504,7 +539,7 @@ def tile_ryeelman_pa_t_kernel(
             p = at(step, MXS)
             if p >= 0:
                 multiply(p)
-            if step < TILES:
+            if SQ_AFTER < 0 and step < TILES:
                 squares_on_scalar(step)
             p = at(step, COS)
             if 0 <= p < PAIRS - 1 and CO_MID:
@@ -527,6 +562,8 @@ def tile_ryeelman_pa_t_kernel(
 
         copies(PAIRS - 3)
         combine(PAIRS - 3)
+        for j in range(COMPONENTS):
+            transpose_words(TILES - 1, j)
         normalise(TILES - 1, 0)
         normalise(TILES - 1, 1)
         quantise(PAIRS - 1, ((0, 1),))

@@ -23,63 +23,36 @@ EPSILON = 1e-6
 PACK = 4
 K_PASS = P * PACK
 PASSES = CHANNELS // K_PASS
+HALVES = COMPONENTS * PASSES
+
 TILES = BATCH // P
 PAIRS = TILES // 2
 QUAD = 4
 QUADS = TILES // QUAD
-LOAD_AHEAD = 4
-HALVES = COMPONENTS * PASSES
+DRAIN_PAIRS = 4
+
 SCALAR_HALVES = 3
-VECTOR_HALVES = 1
-GPSIMD_FIRST = SCALAR_HALVES + VECTOR_HALVES
-WORDS = 3
-LENGTHS = 2
-SQA = 1
-QS = 5
-MXS = 7
-CPS = 8
-MUS = 8
-ADS = 10
-COS = 10
-CP_LATE = False
-CO_MID = True
-SUMS_IN_ACC = True
-ADD = ""
-S_ZERO = 3
-HEAD = 0
-HEAD_S = 2
-HEAD_V = 2
-MIN_S = 2
-INV_VEC = ()
-COL_V = True
-LIN_V = False
-BIAS_DIRECT = True
-INV0_AFTER = 0
-DR_A = 12
-ADD_SLICES = PACK
-EPS_TILE = False
-VE = 0
-VO = 0
-VS = PACK
-G_MERGE = True
-LAST = 0
-INV_L = [0, 2, 6, 10, 14, 18, 22, 26]
-INV_T = [0, 5, 9, 13, 17, 21, 25, 29]
-INV_Q = [1, 6, 10, 14, 18, 22, 26, 30]
-LIN = [7, 9, 11, 15, 19, 23, 27, 31]
-F_LATE = True
-ORDER = [("s", 0, 4), ("r", 0, 0), ("s", 10, 4), ("r", 1, 0), ("x", 0, 0), ("x", 1, 0), ("x", 2, 0)]
-SQ_AFTER = -1
-WARM0 = 0
-WARM_STEPS = {}
-WARM_MX = {}
-W_AT = 1
-XL = 3
+
+LOAD_AHEAD = 4
+LENGTHS_STEP = 2
+NORMALISE_STEP = 3
+QUANTISE_STEP = 5
+MULTIPLY_STEP = 7
+COMBINE_STEP = 8
+ADD_UP_STEP = 10
 
 LEFT, RIGHT, LINEAR = 0, 2, 4
 WEIGHT_SLOTS = 5
 
 FLOPS = 2 * BATCH * HIDDEN * (2 * COMPONENTS * CHANNELS + FEATURES)
+
+
+def quad_step(quad):
+    return 0 if quad == 0 else 4 * quad + 1
+
+
+def linear_step(quad):
+    return max(MULTIPLY_STEP + 2 * quad, 4 * quad + 3)
 
 
 def load_weight(nc, w_codes, w_planes, slot, words, scales):
@@ -119,10 +92,10 @@ def tile_ryeelman_pa_t_kernel(
     with ExitStack() as ctx:
         keep = ctx.enter_context(tc.tile_pool(name="keep", bufs=1))
         inv_pool = ctx.enter_context(tc.tile_pool(name="inv", bufs=3))
-        x_pool = ctx.enter_context(tc.tile_pool(name="x", bufs=LOAD_AHEAD + XL + 1))
+        x_pool = ctx.enter_context(tc.tile_pool(name="x", bufs=LOAD_AHEAD + NORMALISE_STEP + 1))
         work = ctx.enter_context(tc.tile_pool(name="work", bufs=2))
-        words_psum = ctx.enter_context(tc.psum_pool(name="words", bufs=WORDS))
-        lengths_psum = ctx.enter_context(tc.psum_pool(name="lengths", bufs=LENGTHS))
+        words_psum = ctx.enter_context(tc.psum_pool(name="words", bufs=3))
+        lengths_psum = ctx.enter_context(tc.psum_pool(name="lengths", bufs=2))
         acc_psum = ctx.enter_context(tc.psum_pool(name="acc", bufs=1))
         ctx.enter_context(tc.manual_schedule())
 
@@ -131,76 +104,69 @@ def tile_ryeelman_pa_t_kernel(
         w_codes = keep.tile([P, WEIGHT_SLOTS, PACK * HIDDEN], U8, align_bytes=64)
         w_planes = keep.tile([P, WEIGHT_SLOTS, HIDDEN], U8, align_bytes=64)
         nc.vector.memset(w_planes[:].bitcast(I32), 0)
-        zero = keep.tile([P, 1], F32)
-        nc.vector.memset(zero[:], 0.0)
-        epsilon = keep.tile([P, 1], F32)
-        nc.vector.tensor_scalar_add(out=epsilon[:], in0=zero[:], scalar1=EPSILON)
+        one = keep.tile([P, 1], F32)
+        nc.vector.memset(one[:], 1.0)
         table_warmer = keep.tile([P, 1], F32)
-        nc.scalar.activation(out=table_warmer[:], in_=epsilon[:], func=ACT.Abs_reciprocal_sqrt)
+        nc.scalar.activation(out=table_warmer[:], in_=one[:], func=ACT.Abs_reciprocal_sqrt)
         identity = keep.tile([P, P], F32)
         make_identity(nc, identity[:])
         bias_column = keep.tile([P, 1], BF16)
 
-        lin_all = keep.tile([P, TILES, P], F32)
-        z_all = lin_all
+        rows_all = keep.tile([P, TILES, P], F32)
 
-        warm_sb = keep.tile([P, 4 * P], BF16)
-        nc.vector.memset(warm_sb[:], 1.0)
         inv_tiles = {}
-        grouped_tiles = {}
+        inv_turned_tiles = {}
+        inv_operands = {}
+        linear_tiles = {}
         x_tiles = {}
         late_tiles = {}
         early_tiles = {}
-        factor_tiles = {}
-        xn_tiles = {}
-        xT_tiles = {}
         length_tiles = {}
+        factor_tiles = {}
+        word_tiles = {}
+        xn_tiles = {}
         operand_tiles = {}
         product_tiles = {}
         right_tiles = {}
         term_tiles = {}
         sum_tiles = {}
-        lin_tiles = {}
-        inv_operands = {}
 
-        def load_invariants(c):
-            first = c * QUAD
+        def load_invariants(quad):
+            tiles = slice(quad * QUAD, (quad + 1) * QUAD)
             inv_sb = inv_pool.tile([P, QUAD, FEATURES], BF16)
-            nc.sync.dma_start(out=inv_sb[:, :, 0:INPUT_FEATURES], in_=inv_input_rows[:, first : first + QUAD, :])
-            nc.sync.dma_start(out=inv_sb[:, :, INPUT_FEATURES:FEATURES], in_=inv_hidden_rows[:, first : first + QUAD, :])
-            inv_tiles[c] = inv_sb
+            nc.sync.dma_start(out=inv_sb[:, :, 0:INPUT_FEATURES], in_=inv_input_rows[:, tiles, :])
+            nc.sync.dma_start(out=inv_sb[:, :, INPUT_FEATURES:FEATURES], in_=inv_hidden_rows[:, tiles, :])
+            inv_tiles[quad] = inv_sb
 
-        def group_invariants(c):
-            inv_sb = inv_tiles[c]
-            inv_grouped = inv_pool.tile([P, QUAD * P, PACK], BF16, align_bytes=64)
-            grouped_tiles[c] = inv_grouped
+        def turn_invariants(quad):
+            inv_turned = inv_pool.tile([P, QUAD * P, PACK], BF16, align_bytes=64)
             for pair in range(QUAD // 2):
                 invT = words_psum.tile([P, 2, 2 * P], F32, tag="xT")
                 for i in range(2):
-                    inv_words = inv_sb[:, 2 * pair + i, :].bitcast(F32)
+                    inv_words = inv_tiles[quad][:, 2 * pair + i, :].bitcast(F32)
                     for u in range(2):
-                        nc.tensor.transpose(invT[:, u, i * P : (i + 1) * P], inv_words[:, u : FEATURES // 2 : 2], identity[:])
-                grouped_words = inv_grouped[:, 2 * pair * P : 2 * (pair + 1) * P, :].bitcast(F32)
-                if c in INV_VEC:
-                    nc.vector.tensor_copy(out=grouped_words, in_=invT[:].rearrange("p u c -> p c u"))
-                else:
-                    nc.scalar.copy(out=grouped_words, in_=invT[:].rearrange("p u c -> p c u"))
+                        nc.tensor.transpose(
+                            invT[:, u, i * P : (i + 1) * P], inv_words[:, u : FEATURES // 2 : 2], identity[:]
+                        )
+                turned_words = inv_turned[:, 2 * pair * P : 2 * (pair + 1) * P, :].bitcast(F32)
+                nc.scalar.copy(out=turned_words, in_=invT[:].rearrange("p u c -> p c u"))
+            inv_turned_tiles[quad] = inv_turned
 
-        def quantise_invariants(c):
+        def quantise_invariants(quad):
             inv_codes = inv_pool.tile([P, QUAD * P], U32, align_bytes=64)
             inv_planes = inv_pool.tile([P, QUAD * P], U8, align_bytes=64)
-            inv_operands[c] = (inv_codes, inv_planes)
             nc.vector.quantize_mx(
                 out=inv_codes[:].bitcast(FP8X4),
                 scales=inv_planes[:],
-                in_=grouped_tiles[c][:].rearrange("p c t -> p (c t)"),
+                in_=inv_turned_tiles[quad][:].rearrange("p c t -> p (c t)"),
             )
+            inv_operands[quad] = (inv_codes, inv_planes)
 
-        def linear_product(c):
-            inv_codes, inv_planes = inv_operands[c]
-            lin_ps = lengths_psum.tile([P, QUAD * P], F32, tag="small")
+        def linear_product(quad):
+            inv_codes, inv_planes = inv_operands[quad]
+            linear = lengths_psum.tile([P, QUAD * P], F32, tag="small")
             nc.tensor.matmul_mx(
-                out=lin_ps[:],
+                out=linear[:],
                 lhsT=w_codes[:, LINEAR, :].bitcast(FP8X4),
                 lhsT_scale=w_planes[:, LINEAR, :],
                 rhs=inv_codes[:].bitcast(FP8X4),
@@ -208,19 +174,16 @@ def tile_ryeelman_pa_t_kernel(
                 start=True,
                 stop=True,
             )
-            lin_tiles[c] = lin_ps
+            linear_tiles[quad] = linear
 
-        def linear_out(c):
-            first = c * QUAD
-            if LIN_V:
-                nc.vector.tensor_scalar(
-                    out=lin_all[:, first : first + QUAD, :].rearrange("p i b -> p (i b)"), in0=lin_tiles[c][:], scalar1=bias_column[:], scalar2=None, op0=ALU.add,
-                )
-            else:
-                nc.scalar.activation(
-                    out=lin_all[:, first : first + QUAD, :].rearrange("p i b -> p (i b)"),
-                    in_=lin_tiles[c][:], func=ACT.Identity, bias=bias_column[:], scale=1.0,
-                )
+        def linear_terms(quad):
+            nc.scalar.activation(
+                out=rows_all[:, quad * QUAD : (quad + 1) * QUAD, :].rearrange("p i b -> p (i b)"),
+                in_=linear_tiles[quad][:],
+                func=ACT.Identity,
+                bias=bias_column[:],
+                scale=1.0,
+            )
 
         def load(t):
             x_sb = x_pool.tile([P, COMPONENTS, CHANNELS], BF16)
@@ -239,225 +202,156 @@ def tile_ryeelman_pa_t_kernel(
             halves = x_tiles[t][:].rearrange("p j (g c) -> p (j g) c", g=PASSES)
             return halves.rearrange("p a (q k) -> p a k q", k=PACK)
 
-        def split(t):
-            if t == 0:
-                return S_ZERO, HALVES - S_ZERO
-            if t < HEAD:
-                return HEAD_S, HEAD_V
-            return SCALAR_HALVES, VE if t % 2 == 0 else VO
-
-        def squares_on_gpsimd(t):
+        def late_squares(t):
             stepped = stepped_halves(t)
-            late = work.tile([P, HALVES - MIN_S, PACK, P], F32, bufs=SQA + 4)
-            s, v = split(t)
-            early_head = t == 0 or t < HEAD
-            if early_head:
-                nc.vector.tensor_copy(out=x_tiles[t][:, :, 0:1], in_=first_channel[:, t, :].unsqueeze(2))
-            for a in range(s, s + v):
-                vs = PACK if early_head else VS
-                nc.vector.tensor_tensor(out=late[:, a - MIN_S, 0:vs], in0=stepped[:, a, 0:vs], in1=stepped[:, a, 0:vs], op=ALU.mult)
-            if not early_head:
-                nc.vector.tensor_copy(out=x_tiles[t][:, :, 0:1], in_=first_channel[:, t, :].unsqueeze(2))
-            if G_MERGE and s + v < HALVES:
-                nc.gpsimd.tensor_tensor(out=late[:, s + v - MIN_S :], in0=stepped[:, s + v :], in1=stepped[:, s + v :], op=ALU.mult)
-            elif not G_MERGE:
-                for a in range(s + v, HALVES):
-                    nc.gpsimd.tensor_tensor(out=late[:, a - MIN_S], in0=stepped[:, a], in1=stepped[:, a], op=ALU.mult)
-            if VS < PACK and v and not early_head:
-                a = s
-                nc.gpsimd.tensor_tensor(out=late[:, a - MIN_S, VS:], in0=stepped[:, a, VS:], in1=stepped[:, a, VS:], op=ALU.mult)
+            late = work.tile([P, HALVES - SCALAR_HALVES, PACK, P], F32, bufs=5)
+            nc.vector.tensor_copy(out=x_tiles[t][:, :, 0:1], in_=first_channel[:, t, :].unsqueeze(2))
+            if t == 0:
+                for a in range(SCALAR_HALVES, HALVES):
+                    nc.vector.tensor_tensor(
+                        out=late[:, a - SCALAR_HALVES], in0=stepped[:, a], in1=stepped[:, a], op=ALU.mult
+                    )
+            else:
+                nc.gpsimd.tensor_tensor(
+                    out=late[:], in0=stepped[:, SCALAR_HALVES:], in1=stepped[:, SCALAR_HALVES:], op=ALU.mult
+                )
             late_tiles[t] = late
-            if ADD == "G":
-                add_squares(nc.gpsimd, t)
 
-        def add_squares(engine, t):
-            late = late_tiles[t]
-            a, b = 3 - MIN_S, 5 - MIN_S
-            engine.tensor_tensor(out=late[:, b, 0:ADD_SLICES], in0=late[:, a, 0:ADD_SLICES], in1=late[:, b, 0:ADD_SLICES], op=ALU.add)
-
-        def squares_on_scalar(t):
-            s = split(t)[0]
+        def early_squares(t):
             early = work.tile([P, SCALAR_HALVES, PACK, P], F32, bufs=4)
-            nc.scalar.activation(out=early[:, 0:s], in_=stepped_halves(t)[:, 0:s], func=ACT.Square)
+            nc.scalar.activation(out=early[:], in_=stepped_halves(t)[:, 0:SCALAR_HALVES], func=ACT.Square)
             early_tiles[t] = early
 
-        def open_lengths(t):
-            factor_tiles[t] = work.tile([P, PASSES, P, PACK], F32, name="inv_length")
-
-        def sum_squares(t, g, k):
+        def inverse_lengths(t):
             early, late = early_tiles[t], late_tiles[t]
-            if k == 0:
-                length_tiles[t, g] = lengths_psum.tile([P, PACK, P], F32, name="length2T", tag="small")
-            for j in range(COMPONENTS):
-                half = PASSES * j + g
-                if half == 3 and ADD and k < ADD_SLICES:
-                    continue
-                if half < split(t)[0]:
-                    source = early[:, half, k, :]
-                else:
-                    source = late[:, half - MIN_S, k, :]
-                nc.tensor.matmul(
-                    out=length_tiles[t, g][:, k, :],
-                    lhsT=source,
-                    rhs=identity[:],
-                    is_transpose=True,
-                    start=(j == 0),
-                    stop=(j == COMPONENTS - 1),
+            inv_length = work.tile([P, PASSES, P, PACK], F32)
+            for g in range(PASSES):
+                length2T = lengths_psum.tile([P, PACK, P], F32, tag="small")
+                for k in range(PACK):
+                    for j in range(COMPONENTS):
+                        half = PASSES * j + g
+                        if half < SCALAR_HALVES:
+                            source = early[:, half, k, :]
+                        else:
+                            source = late[:, half - SCALAR_HALVES, k, :]
+                        nc.tensor.matmul(
+                            out=length2T[:, k, :],
+                            lhsT=source,
+                            rhs=identity[:],
+                            is_transpose=True,
+                            start=(j == 0),
+                            stop=(j == COMPONENTS - 1),
+                        )
+                nc.scalar.activation(
+                    out=inv_length[:, g],
+                    in_=length2T[:].rearrange("p k b -> p b k"),
+                    func=ACT.Abs_reciprocal_sqrt,
+                    bias=EPSILON,
+                    scale=1.0,
                 )
+            length_tiles[t] = inv_length
 
-        def inverse_lengths(t, g):
-            nc.scalar.activation(
-                out=factor_tiles[t][:, g],
-                in_=length_tiles[t, g][:].rearrange("p k b -> p b k"),
-                func=ACT.Abs_reciprocal_sqrt,
-                bias=epsilon[:] if EPS_TILE else EPSILON,
-                scale=1.0,
-            )
-
-        def square_factor(t):
-            factor = work.tile([P, PASSES, P, PACK], F32, bufs=XL)
-            nc.scalar.activation(out=factor[:], in_=factor_tiles[t][:], func=ACT.Square)
+        def factors(t):
+            factor = work.tile([P, PASSES, P, PACK], F32, bufs=3)
+            nc.scalar.activation(out=factor[:], in_=length_tiles[t][:], func=ACT.Square)
             factor_tiles[t] = factor
 
-        def transpose_word(t, j, g, u):
-            if g == 0 and u == 0:
-                xT_tiles[t, j] = words_psum.tile([P, 2, PASSES * P], F32, tag="xT", name="xT")
-            x_words = x_tiles[t][:, j, :].bitcast(F32)
-            nc.tensor.transpose(
-                xT_tiles[t, j][:, u, g * P : (g + 1) * P],
-                x_words[:, g * 2 * P + u : (g + 1) * 2 * P : 2],
-                identity[:],
-            )
-
         def transpose_words(t, j):
+            xT = words_psum.tile([P, 2, PASSES * P], F32, tag="xT")
+            x_words = x_tiles[t][:, j, :].bitcast(F32)
             for g in range(PASSES):
                 for u in range(2):
-                    transpose_word(t, j, g, u)
+                    nc.tensor.transpose(
+                        xT[:, u, g * P : (g + 1) * P],
+                        x_words[:, g * 2 * P + u : (g + 1) * 2 * P : 2],
+                        identity[:],
+                    )
+            word_tiles[t, j] = xT
 
         def normalise(t, j):
-            factor = factor_tiles[t]
-            i = t % 2
-            if i == 0 and j == 0:
-                xn_tiles[t // 2] = work.tile([P, COMPONENTS, PASSES, 2, P * PACK], BF16, align_bytes=64, name="xn")
-            xn = xn_tiles[t // 2]
-            xT = xT_tiles[t, j]
+            if t % 2 == 0 and j == 0:
+                xn01 = work.tile([P, PASSES, 2, 2, P * PACK], BF16, align_bytes=64)
+                xn2 = work.tile([P, PASSES, 2, P * PACK], BF16, align_bytes=64)
+                xn_tiles[t // 2] = (xn01, xn2)
+            xn01, xn2 = xn_tiles[t // 2]
+            xn = xn01[:, :, j, t % 2, :] if j < 2 else xn2[:, :, t % 2, :]
             nc.vector.tensor_tensor(
-                out=xn[:, j, :, i, :].rearrange("p g (b u e) -> p g b u e", u=2, e=2),
-                in0=xT[:].bitcast(BF16).rearrange("p u (g b e) -> p g b u e", g=PASSES, e=2),
-                in1=factor[:].rearrange("p g b (u e) -> p g b u e", e=2),
+                out=xn.rearrange("p g (b u e) -> p g b u e", u=2, e=2),
+                in0=word_tiles[t, j][:].bitcast(BF16).rearrange("p u (g b e) -> p g b u e", g=PASSES, e=2),
+                in1=factor_tiles[t][:].rearrange("p g b (u e) -> p g b u e", e=2),
                 op=ALU.mult,
             )
 
-        def keep_clock(n):
-            warm_ps = lengths_psum.tile([P, 4 * P], F32, tag="small")
-            for i in range(n):
-                nc.tensor.matmul(out=warm_ps[:], lhsT=warm_sb[:, 0:P], rhs=warm_sb[:], start=True, stop=True)
+        def quantise01(pair):
+            codes01 = work.tile([P, PASSES, 4 * P], U32, align_bytes=64)
+            planes01 = work.tile([P, PASSES, 4 * P], U8, align_bytes=64)
+            nc.vector.quantize_mx(
+                out=codes01[:].rearrange("p g c -> p (g c)").bitcast(FP8X4),
+                scales=planes01[:].rearrange("p g c -> p (g c)"),
+                in_=xn_tiles[pair][0][:].rearrange("p g j i c -> p (g j i c)"),
+            )
+            operand_tiles[pair, 0] = (codes01, planes01)
 
-        def keep_clock_mx(n):
-            warm_ps = lengths_psum.tile([P, 4 * P], F32, tag="small")
-            inv_codes, inv_planes = inv_operands[0]
-            for i in range(n):
-                nc.tensor.matmul_mx(out=warm_ps[:], lhsT=w_codes[:, LINEAR, :].bitcast(FP8X4), lhsT_scale=w_planes[:, LINEAR, :], rhs=inv_codes[:].bitcast(FP8X4), rhs_scale=inv_planes[:], start=True, stop=True)
+        def quantise2(pair):
+            codes2 = work.tile([P, PASSES, 2 * P], U32, align_bytes=64)
+            planes2 = work.tile([P, PASSES, 2 * P], U8, align_bytes=64)
+            nc.vector.quantize_mx(
+                out=codes2[:].rearrange("p g c -> p (g c)").bitcast(FP8X4),
+                scales=planes2[:].rearrange("p g c -> p (g c)"),
+                in_=xn_tiles[pair][1][:].rearrange("p g i c -> p (g i c)"),
+            )
+            operand_tiles[pair, 2] = (codes2, planes2)
 
-        def transposes(ts, tx, new):
-            sums = 0 <= ts < TILES
-            words = 0 <= tx < TILES
-            if sums:
-                open_lengths(ts)
-            for kind, a, b in ORDER:
-                if kind == "s" and sums:
-                    for k in range(a % 10, b):
-                        sum_squares(ts, a // 10, k)
-                if kind == "r":
-                    if sums:
-                        inverse_lengths(ts, a)
-                    if a == SQ_AFTER and new < TILES:
-                        squares_on_scalar(new)
-                if kind == "x" and words:
-                    transpose_words(tx, a)
-                    normalise(tx, a)
-                if kind == "f" and sums:
-                    square_factor(ts)
-
-        def quantise(p, components):
-            xn = xn_tiles[p]
-            if p not in operand_tiles:
-                xn_codes = work.tile([P, COMPONENTS, PASSES, 2 * P], U32, align_bytes=64)
-                xn_planes = work.tile([P, COMPONENTS, PASSES, 2 * P], U8, align_bytes=64)
-                operand_tiles[p] = (xn_codes, xn_planes)
-            xn_codes, xn_planes = operand_tiles[p]
-            for first, last in components:
-                nc.vector.quantize_mx(
-                    out=xn_codes[:, first:last].rearrange("p j g c -> p (j g c)").bitcast(FP8X4),
-                    scales=xn_planes[:, first:last].rearrange("p j g c -> p (j g c)"),
-                    in_=xn[:, first:last].rearrange("p j g i c -> p (j g i c)"),
-                )
-
-        def multiply(p):
-            xn_codes, xn_planes = operand_tiles[p]
-            if p < PAIRS - 1:
-                right01 = acc_psum.tile([P, 2, 2 * P], F32, tag="right01")
+        def multiply(pair):
+            if pair < PAIRS - 1:
+                right01 = acc_psum.tile([P, 2 * 2 * P], F32, tag="right01")
                 both2 = acc_psum.tile([P, 2, 2 * P], F32, tag="both2")
-                left01 = acc_psum.tile([P, 2, 2 * P], F32, tag="left01")
+                left01 = acc_psum.tile([P, 2 * 2 * P], F32, tag="left01")
             else:
-                right01 = words_psum.tile([P, 2, 2 * P], F32, tag="xT")
-                left01 = words_psum.tile([P, 2, 2 * P], F32, tag="xT")
+                right01 = words_psum.tile([P, 2 * 2 * P], F32, tag="xT")
+                left01 = words_psum.tile([P, 2 * 2 * P], F32, tag="xT")
                 both2 = words_psum.tile([P, 2, 2 * P], F32, tag="xT")
-            order = [
-                (RIGHT, 0, right01, 0),
-                (RIGHT, 1, right01, 1),
-                (RIGHT, 2, both2, 0),
-                (LEFT, 2, both2, 1),
-                (LEFT, 0, left01, 0),
-                (LEFT, 1, left01, 1),
-            ]
-            if p == PAIRS - 1:
-                order = [order[i] for i in (0, 4, 1, 5, 2, 3)]
-            for side, j, acc, slot in order:
+            products = ((RIGHT, 0, right01[:]), (RIGHT, 2, both2[:, 0, :]), (LEFT, 2, both2[:, 1, :]), (LEFT, 0, left01[:]))
+            if pair == PAIRS - 1:
+                products = (products[0], products[3], products[1], products[2])
+            for side, j, acc in products:
+                codes, planes = operand_tiles[pair, j]
                 for g in range(PASSES):
                     nc.tensor.matmul_mx(
-                        out=acc[:, slot, :],
+                        out=acc,
                         lhsT=w_codes[:, side + g, :].bitcast(FP8X4),
                         lhsT_scale=w_planes[:, side + g, :],
-                        rhs=xn_codes[:, j, g, :].bitcast(FP8X4),
-                        rhs_scale=xn_planes[:, j, g, :],
+                        rhs=codes[:, g, :].bitcast(FP8X4),
+                        rhs_scale=planes[:, g, :],
                         start=(g == 0),
                         stop=(g == PASSES - 1),
                     )
-            product_tiles[p] = (right01, both2, left01)
+            product_tiles[pair] = (right01, both2, left01)
 
-        def copies(p):
-            right01, both2, left01 = product_tiles[p]
+        def copy_right(pair):
+            right01, both2, left01 = product_tiles[pair]
             right_sb = work.tile([P, COMPONENTS, 2 * P], F32)
-            nc.scalar.copy(out=right_sb[:, 0:2, :], in_=right01[:])
+            nc.scalar.copy(out=right_sb[:, 0:2, :].rearrange("p j c -> p (j c)"), in_=right01[:])
             nc.scalar.copy(out=right_sb[:, 2, :], in_=both2[:, 0, :])
-            right_tiles[p] = right_sb
+            right_tiles[pair] = right_sb
 
-        def combine(p):
-            right01, both2, left01 = product_tiles[p]
-            right_sb = right_tiles[p]
+        def combine(pair):
+            right01, both2, left01 = product_tiles[pair]
+            right_sb = right_tiles[pair]
             terms = work.tile([P, COMPONENTS, 2, P], F32)
-            def third():
-                nc.vector.tensor_tensor(
-                    out=terms[:, 2].rearrange("p i b -> p (i b)"), in0=both2[:, 1, :], in1=right_sb[:, 2, :], op=ALU.mult
-                )
-            if p < PAIRS - 1:
-                third()
-            nc.vector.tensor_tensor(
-                out=terms[:, 0:2].rearrange("p j i b -> p j (i b)"), in0=left01[:], in1=right_sb[:, 0:2, :], op=ALU.mult
-            )
-            if p == PAIRS - 1:
-                third()
-            term_tiles[p] = terms
+            thirds = (terms[:, 2].rearrange("p i b -> p (i b)"), both2[:, 1, :], right_sb[:, 2, :])
+            others = (terms[:, 0:2].rearrange("p j i b -> p (j i b)"), left01[:], right_sb[:, 0:2, :].rearrange("p j c -> p (j c)"))
+            for product, left, right in (thirds, others) if pair < PAIRS - 1 else (others, thirds):
+                nc.vector.tensor_tensor(out=product, in0=left, in1=right, op=ALU.mult)
+            term_tiles[pair] = terms
 
-        def add_up(p):
-            terms = term_tiles[p]
-            if p < PAIRS - 4:
+        def add_up(pair):
+            if pair < PAIRS - DRAIN_PAIRS:
                 sums = acc_psum.tile([P, 2, HIDDEN], F32, tag="right01")
             else:
                 sums = lengths_psum.tile([P, 2, HIDDEN], F32, tag="small")
             for i in range(2):
-                sources = [lin_all[:, 2 * p + i, :]] + [terms[:, j, i, :] for j in range(COMPONENTS)]
+                sources = [rows_all[:, 2 * pair + i, :]] + [term_tiles[pair][:, j, i, :] for j in range(COMPONENTS)]
                 for s in range(len(sources)):
                     nc.tensor.matmul(
                         out=sums[:, i, :],
@@ -467,123 +361,107 @@ def tile_ryeelman_pa_t_kernel(
                         start=(s == 0),
                         stop=(s == COMPONENTS),
                     )
-            sum_tiles[p] = sums
+            sum_tiles[pair] = sums
 
-        def collect(p):
-            if p < PAIRS - 4:
-                if COL_V:
-                    nc.vector.tensor_copy(out=z_all[:, 2 * p : 2 * p + 2, :], in_=sum_tiles[p][:])
-                else:
-                    nc.scalar.copy(out=z_all[:, 2 * p : 2 * p + 2, :], in_=sum_tiles[p][:])
-            else:
-                nc.scalar.activation(out=z_all[:, 2 * p : 2 * p + 2, :], in_=sum_tiles[p][:], func=ACT.Tanh)
+        def collect(pair):
+            nc.vector.tensor_copy(out=rows_all[:, 2 * pair : 2 * pair + 2, :], in_=sum_tiles[pair][:])
+
+        def collect_tanh(pair):
+            nc.scalar.activation(out=rows_all[:, 2 * pair : 2 * pair + 2, :], in_=sum_tiles[pair][:], func=ACT.Tanh)
+
+        def store(begin, end):
+            nc.sync.dma_start(out=out_rows[:, begin:end, :], in_=rows_all[:, begin:end, :])
 
         def finish(begin, end):
-            nc.scalar.activation(out=z_all[:, begin:end, :], in_=z_all[:, begin:end, :], func=ACT.Tanh)
-            nc.sync.dma_start(out=out_rows[:, begin:end, :], in_=z_all[:, begin:end, :])
+            nc.scalar.activation(out=rows_all[:, begin:end, :], in_=rows_all[:, begin:end, :], func=ACT.Tanh)
+            store(begin, end)
+
+        def due(step, stage):
+            pair, rest = divmod(step - stage, 2)
+            return pair if rest == 0 and 0 <= pair < PAIRS else None
 
         for t in range(LOAD_AHEAD):
             load(t)
-            if INV_L[0] == 0 and t == INV0_AFTER:
+            if t == 0:
                 load_invariants(0)
-        for t in range(SQA):
-            squares_on_gpsimd(t)
+        late_squares(0)
 
-        def at(step, lag):
-            q, r = divmod(step - lag - XL + 3, 2)
-            return q if r == 0 and 0 <= q < PAIRS else -1
-
-        if WARM0:
-            keep_clock(WARM0)
-        for step in range(TILES + XL - 1):
-            if WARM_STEPS.get(step, 0):
-                keep_clock(WARM_STEPS[step])
-            if WARM_MX.get(step, 0):
-                keep_clock_mx(WARM_MX[step])
+        quad_by_step = {quad_step(quad): quad for quad in range(QUADS)}
+        linear_by_step = {linear_step(quad): quad for quad in range(QUADS)}
+        for step in range(TILES + LENGTHS_STEP):
             if step + LOAD_AHEAD < TILES:
                 load(step + LOAD_AHEAD)
-            for c in range(QUADS):
-                if INV_L[c] and step + 1 == INV_L[c]:
-                    load_invariants(c)
-            if step == W_AT:
+            if step + LOAD_AHEAD in quad_by_step:
+                load_invariants(quad_by_step[step + LOAD_AHEAD])
+            if step == 1:
                 load_weight(nc, w_codes, w_planes, LINEAR, W_ii_words, W_ii_scales)
                 load_weight(nc, w_codes, w_planes, LEFT, W_left_words, W_left_scales)
                 load_weight(nc, w_codes, w_planes, RIGHT, W_right_words, W_right_scales)
                 nc.sync.dma_start(out=bias_column[:], in_=b_ii.rearrange("(h o) -> h o", o=1))
-            p = at(step, COS)
-            if 0 <= p < PAIRS - 1 and not CO_MID:
-                collect(p)
-            p = at(step, CPS)
-            if p >= 0 and not CP_LATE:
-                copies(p)
-            p = at(step, MUS)
-            if p >= 0 and not CP_LATE:
-                combine(p)
-            transposes(step - 2, step - XL, step)
-            p = at(step, ADS)
-            if p >= 0:
-                add_up(p)
-            p = at(step, QS)
-            if p >= 0:
-                quantise(p, ((0, 2), (2, 3)))
-            if step + SQA < TILES:
-                squares_on_gpsimd(step + SQA)
-            elif ADD == "V" and step + SQA == TILES:
-                add_squares(nc.vector, TILES - 1)
-            for c in range(QUADS):
-                if step == INV_Q[c]:
-                    quantise_invariants(c)
-            for c in range(QUADS):
-                if step == LIN[c]:
-                    linear_product(c)
-            p = at(step, MXS)
-            if p >= 0:
-                multiply(p)
-            if SQ_AFTER < 0 and step < TILES:
-                squares_on_scalar(step)
-            p = at(step, COS)
-            if 0 <= p < PAIRS - 1 and CO_MID:
-                collect(p)
-            t = step - 2
-            if F_LATE and 0 <= t < TILES:
-                square_factor(t)
-            for c in range(QUADS):
-                if step == LIN[c]:
-                    linear_out(c)
-            for c in range(QUADS):
-                if step == INV_T[c]:
-                    group_invariants(c)
-            p = at(step, CPS)
-            if p >= 0 and CP_LATE:
-                copies(p)
-            p = at(step, MUS)
-            if p >= 0 and CP_LATE:
-                combine(p)
+            pair = due(step, COMBINE_STEP)
+            if pair is not None:
+                copy_right(pair)
+                combine(pair)
+            if 0 <= step - LENGTHS_STEP < TILES:
+                inverse_lengths(step - LENGTHS_STEP)
+            if 0 <= step - NORMALISE_STEP < TILES:
+                for j in range(COMPONENTS):
+                    transpose_words(step - NORMALISE_STEP, j)
+                    normalise(step - NORMALISE_STEP, j)
+            pair = due(step, ADD_UP_STEP)
+            if pair is not None:
+                add_up(pair)
+            pair = due(step, QUANTISE_STEP)
+            if pair is not None:
+                quantise01(pair)
+                quantise2(pair)
+            if step + 1 < TILES:
+                late_squares(step + 1)
+            if step - 1 in quad_by_step:
+                quantise_invariants(quad_by_step[step - 1])
+            if step in linear_by_step:
+                linear_product(linear_by_step[step])
+            pair = due(step, MULTIPLY_STEP)
+            if pair is not None:
+                multiply(pair)
+            if step < TILES:
+                early_squares(step)
+            pair = due(step, ADD_UP_STEP)
+            if pair is not None:
+                collect(pair)
+            if 0 <= step - LENGTHS_STEP < TILES:
+                factors(step - LENGTHS_STEP)
+            if step in linear_by_step:
+                linear_terms(linear_by_step[step])
+            if step in quad_by_step:
+                turn_invariants(quad_by_step[step])
 
-        copies(PAIRS - 3)
-        combine(PAIRS - 3)
+        last_tile, last_pair = TILES - 1, PAIRS - 1
+        stored = TILES - 2 * DRAIN_PAIRS
+        copy_right(last_pair - 2)
+        combine(last_pair - 2)
         for j in range(COMPONENTS):
-            transpose_words(TILES - 1, j)
-        normalise(TILES - 1, 0)
-        normalise(TILES - 1, 1)
-        quantise(PAIRS - 1, ((0, 1),))
-        normalise(TILES - 1, 2)
-        add_up(PAIRS - 4)
-        multiply(PAIRS - 2)
-        collect(PAIRS - 4)
-        finish(0, DR_A)
-        copies(PAIRS - 2)
-        quantise(PAIRS - 1, ((1, 2), (2, 3)))
-        combine(PAIRS - 2)
-        add_up(PAIRS - 3)
-        multiply(PAIRS - 1)
-        collect(PAIRS - 3)
-        finish(DR_A, TILES - 8)
-        add_up(PAIRS - 2)
-        copies(PAIRS - 1)
-        collect(PAIRS - 2)
-        nc.sync.dma_start(out=out_rows[:, TILES - 8 : TILES - 2, :], in_=z_all[:, TILES - 8 : TILES - 2, :])
-        combine(PAIRS - 1)
-        add_up(PAIRS - 1)
-        collect(PAIRS - 1)
-        nc.sync.dma_start(out=out_rows[:, TILES - 2 :, :], in_=z_all[:, TILES - 2 :, :])
+            transpose_words(last_tile, j)
+        normalise(last_tile, 0)
+        normalise(last_tile, 1)
+        quantise01(last_pair)
+        normalise(last_tile, 2)
+        add_up(last_pair - 3)
+        multiply(last_pair - 1)
+        collect_tanh(last_pair - 3)
+        finish(0, stored // 2)
+        copy_right(last_pair - 1)
+        quantise2(last_pair)
+        combine(last_pair - 1)
+        add_up(last_pair - 2)
+        multiply(last_pair)
+        collect_tanh(last_pair - 2)
+        finish(stored // 2, stored)
+        add_up(last_pair - 1)
+        copy_right(last_pair)
+        collect_tanh(last_pair - 1)
+        store(stored, TILES - 2)
+        combine(last_pair)
+        add_up(last_pair)
+        collect_tanh(last_pair)
+        store(TILES - 2, TILES)

from contextlib import ExitStack

import concourse.mybir as mybir
from concourse.masks import make_identity

F32 = mybir.dt.float32
BF16 = mybir.dt.bfloat16
I32 = mybir.dt.int32
U32 = mybir.dt.uint32
U8 = mybir.dt.uint8
FP8X4 = mybir.dt.float8_e4m3fn_x4
ACT = mybir.ActivationFunctionType
ALU = mybir.AluOpType

P = 128
BATCH = 4096
COMPONENTS = 3
CHANNELS = 1024
INPUT_FEATURES = 384
FEATURES = 512
HIDDEN = 128
EPSILON = 1e-6
PACK = 4
K_PASS = P * PACK
PASSES = CHANNELS // K_PASS
HALVES = COMPONENTS * PASSES

TILES = BATCH // P
PAIRS = TILES // 2
QUAD = 4
QUADS = TILES // QUAD
DRAIN_PAIRS = 4

SCALAR_HALVES = 3

LOAD_AHEAD = 4
LENGTHS_STEP = 2
NORMALISE_STEP = 3
QUANTISE_STEP = 5
MULTIPLY_STEP = 7
COMBINE_STEP = 8
ADD_UP_STEP = 10

LEFT, RIGHT, LINEAR = 0, 2, 4
WEIGHT_SLOTS = 5

FLOPS = 2 * BATCH * HIDDEN * (2 * COMPONENTS * CHANNELS + FEATURES)


def quad_step(quad):
    return 0 if quad == 0 else 4 * quad + 1


def linear_step(quad):
    return max(MULTIPLY_STEP + 2 * quad, 4 * quad + 3)


def load_weight(nc, w_codes, w_planes, slot, words, scales):
    passes = words.shape[0]
    nc.sync.dma_start(
        out=w_codes[:, slot : slot + passes, :].bitcast(I32),
        in_=words.rearrange("g p n t -> p g (n t)").bitcast(I32),
    )
    for quadrant in range(4):
        nc.sync.dma_start(
            out=w_planes[32 * quadrant : 32 * quadrant + 4, slot : slot + passes, :].bitcast(I32),
            in_=scales[:, 4 * quadrant : 4 * quadrant + 4, :].rearrange("g r n -> r g n").bitcast(I32),
        )


def tile_ryeelman_pa_t_kernel(
    tc,
    invariant_input,
    equivariant_input,
    invariant_hidden,
    equivariant_hidden,
    W_left_words,
    W_left_scales,
    W_right_words,
    W_right_scales,
    W_ii_words,
    W_ii_scales,
    b_ii,
    out,
):
    nc = tc.nc
    hidden_runs = equivariant_hidden.rearrange("(p t) j c -> p (t j c)", t=TILES)
    inv_input_rows = invariant_input.rearrange("(p t) k -> p t k", t=TILES)
    inv_hidden_rows = invariant_hidden.rearrange("(p t) k -> p t k", t=TILES)
    out_rows = out.rearrange("(p t) h -> p t h", t=TILES)

    with ExitStack() as ctx:
        keep = ctx.enter_context(tc.tile_pool(name="keep", bufs=1))
        inv_pool = ctx.enter_context(tc.tile_pool(name="inv", bufs=3))
        x_pool = ctx.enter_context(tc.tile_pool(name="x", bufs=LOAD_AHEAD + NORMALISE_STEP + 1))
        work = ctx.enter_context(tc.tile_pool(name="work", bufs=2))
        words_psum = ctx.enter_context(tc.psum_pool(name="words", bufs=3))
        lengths_psum = ctx.enter_context(tc.psum_pool(name="lengths", bufs=2))
        acc_psum = ctx.enter_context(tc.psum_pool(name="acc", bufs=1))
        ctx.enter_context(tc.manual_schedule())

        first_channel = keep.tile([P, TILES, COMPONENTS], BF16)
        nc.sync.dma_start(out=first_channel[:], in_=equivariant_input.rearrange("(p t) j -> p t j", t=TILES))
        w_codes = keep.tile([P, WEIGHT_SLOTS, PACK * HIDDEN], U8, align_bytes=64)
        w_planes = keep.tile([P, WEIGHT_SLOTS, HIDDEN], U8, align_bytes=64)
        nc.vector.memset(w_planes[:].bitcast(I32), 0)
        one = keep.tile([P, 1], F32)
        nc.vector.memset(one[:], 1.0)
        table_warmer = keep.tile([P, 1], F32)
        nc.scalar.activation(out=table_warmer[:], in_=one[:], func=ACT.Abs_reciprocal_sqrt)
        identity = keep.tile([P, P], F32)
        make_identity(nc, identity[:])
        bias_column = keep.tile([P, 1], BF16)

        rows_all = keep.tile([P, TILES, P], F32)

        inv_tiles = {}
        inv_turned_tiles = {}
        inv_operands = {}
        linear_tiles = {}
        x_tiles = {}
        late_tiles = {}
        early_tiles = {}
        length_tiles = {}
        factor_tiles = {}
        word_tiles = {}
        xn_tiles = {}
        operand_tiles = {}
        product_tiles = {}
        right_tiles = {}
        term_tiles = {}
        sum_tiles = {}

        def load_invariants(quad):
            tiles = slice(quad * QUAD, (quad + 1) * QUAD)
            inv_sb = inv_pool.tile([P, QUAD, FEATURES], BF16)
            nc.sync.dma_start(out=inv_sb[:, :, 0:INPUT_FEATURES], in_=inv_input_rows[:, tiles, :])
            nc.sync.dma_start(out=inv_sb[:, :, INPUT_FEATURES:FEATURES], in_=inv_hidden_rows[:, tiles, :])
            inv_tiles[quad] = inv_sb

        def turn_invariants(quad):
            inv_turned = inv_pool.tile([P, QUAD * P, PACK], BF16, align_bytes=64)
            for pair in range(QUAD // 2):
                invT = words_psum.tile([P, 2, 2 * P], F32, tag="xT")
                for i in range(2):
                    inv_words = inv_tiles[quad][:, 2 * pair + i, :].bitcast(F32)
                    for u in range(2):
                        nc.tensor.transpose(
                            invT[:, u, i * P : (i + 1) * P], inv_words[:, u : FEATURES // 2 : 2], identity[:]
                        )
                turned_words = inv_turned[:, 2 * pair * P : 2 * (pair + 1) * P, :].bitcast(F32)
                nc.scalar.copy(out=turned_words, in_=invT[:].rearrange("p u c -> p c u"))
            inv_turned_tiles[quad] = inv_turned

        def quantise_invariants(quad):
            inv_codes = inv_pool.tile([P, QUAD * P], U32, align_bytes=64)
            inv_planes = inv_pool.tile([P, QUAD * P], U8, align_bytes=64)
            nc.vector.quantize_mx(
                out=inv_codes[:].bitcast(FP8X4),
                scales=inv_planes[:],
                in_=inv_turned_tiles[quad][:].rearrange("p c t -> p (c t)"),
            )
            inv_operands[quad] = (inv_codes, inv_planes)

        def linear_product(quad):
            inv_codes, inv_planes = inv_operands[quad]
            linear = lengths_psum.tile([P, QUAD * P], F32, tag="small")
            nc.tensor.matmul_mx(
                out=linear[:],
                lhsT=w_codes[:, LINEAR, :].bitcast(FP8X4),
                lhsT_scale=w_planes[:, LINEAR, :],
                rhs=inv_codes[:].bitcast(FP8X4),
                rhs_scale=inv_planes[:],
                start=True,
                stop=True,
            )
            linear_tiles[quad] = linear

        def linear_terms(quad):
            nc.scalar.activation(
                out=rows_all[:, quad * QUAD : (quad + 1) * QUAD, :].rearrange("p i b -> p (i b)"),
                in_=linear_tiles[quad][:],
                func=ACT.Identity,
                bias=bias_column[:],
                scale=1.0,
            )

        def load(t):
            x_sb = x_pool.tile([P, COMPONENTS, CHANNELS], BF16)
            for j in range(COMPONENTS):
                first = (t * COMPONENTS + j) * (CHANNELS - 1)
                if first == 0:
                    row_raw = keep.tile([P, 8 + CHANNELS], BF16)
                    nc.vector.memset(row_raw[:, 0:8], 0.0)
                    nc.sync.dma_start(out=row_raw[:, 8 : 8 + CHANNELS - 1], in_=hidden_runs[:, 0 : CHANNELS - 1])
                    nc.vector.tensor_copy(out=x_sb[:, j, :], in_=row_raw[:, 7 : 7 + CHANNELS])
                else:
                    nc.sync.dma_start(out=x_sb[:, j, :], in_=hidden_runs[:, first - 1 : first - 1 + CHANNELS])
            x_tiles[t] = x_sb

        def stepped_halves(t):
            halves = x_tiles[t][:].rearrange("p j (g c) -> p (j g) c", g=PASSES)
            return halves.rearrange("p a (q k) -> p a k q", k=PACK)

        def late_squares(t):
            stepped = stepped_halves(t)
            late = work.tile([P, HALVES - SCALAR_HALVES, PACK, P], F32, bufs=5)
            nc.vector.tensor_copy(out=x_tiles[t][:, :, 0:1], in_=first_channel[:, t, :].unsqueeze(2))
            if t == 0:
                for a in range(SCALAR_HALVES, HALVES):
                    nc.vector.tensor_tensor(
                        out=late[:, a - SCALAR_HALVES], in0=stepped[:, a], in1=stepped[:, a], op=ALU.mult
                    )
            else:
                nc.gpsimd.tensor_tensor(
                    out=late[:], in0=stepped[:, SCALAR_HALVES:], in1=stepped[:, SCALAR_HALVES:], op=ALU.mult
                )
            late_tiles[t] = late

        def early_squares(t):
            early = work.tile([P, SCALAR_HALVES, PACK, P], F32, bufs=4)
            nc.scalar.activation(out=early[:], in_=stepped_halves(t)[:, 0:SCALAR_HALVES], func=ACT.Square)
            early_tiles[t] = early

        def inverse_lengths(t):
            early, late = early_tiles[t], late_tiles[t]
            inv_length = work.tile([P, PASSES, P, PACK], F32)
            for g in range(PASSES):
                length2T = lengths_psum.tile([P, PACK, P], F32, tag="small")
                for k in range(PACK):
                    for j in range(COMPONENTS):
                        half = PASSES * j + g
                        if half < SCALAR_HALVES:
                            source = early[:, half, k, :]
                        else:
                            source = late[:, half - SCALAR_HALVES, k, :]
                        nc.tensor.matmul(
                            out=length2T[:, k, :],
                            lhsT=source,
                            rhs=identity[:],
                            is_transpose=True,
                            start=(j == 0),
                            stop=(j == COMPONENTS - 1),
                        )
                nc.scalar.activation(
                    out=inv_length[:, g],
                    in_=length2T[:].rearrange("p k b -> p b k"),
                    func=ACT.Abs_reciprocal_sqrt,
                    bias=EPSILON,
                    scale=1.0,
                )
            length_tiles[t] = inv_length

        def factors(t):
            factor = work.tile([P, PASSES, P, PACK], F32, bufs=3)
            nc.scalar.activation(out=factor[:], in_=length_tiles[t][:], func=ACT.Square)
            factor_tiles[t] = factor

        def transpose_words(t, j):
            xT = words_psum.tile([P, 2, PASSES * P], F32, tag="xT")
            x_words = x_tiles[t][:, j, :].bitcast(F32)
            for g in range(PASSES):
                for u in range(2):
                    nc.tensor.transpose(
                        xT[:, u, g * P : (g + 1) * P],
                        x_words[:, g * 2 * P + u : (g + 1) * 2 * P : 2],
                        identity[:],
                    )
            word_tiles[t, j] = xT

        def normalise(t, j):
            if t % 2 == 0 and j == 0:
                xn01 = work.tile([P, PASSES, 2, 2, P * PACK], BF16, align_bytes=64)
                xn2 = work.tile([P, PASSES, 2, P * PACK], BF16, align_bytes=64)
                xn_tiles[t // 2] = (xn01, xn2)
            xn01, xn2 = xn_tiles[t // 2]
            xn = xn01[:, :, j, t % 2, :] if j < 2 else xn2[:, :, t % 2, :]
            nc.vector.tensor_tensor(
                out=xn.rearrange("p g (b u e) -> p g b u e", u=2, e=2),
                in0=word_tiles[t, j][:].bitcast(BF16).rearrange("p u (g b e) -> p g b u e", g=PASSES, e=2),
                in1=factor_tiles[t][:].rearrange("p g b (u e) -> p g b u e", e=2),
                op=ALU.mult,
            )

        def quantise01(pair):
            codes01 = work.tile([P, PASSES, 4 * P], U32, align_bytes=64)
            planes01 = work.tile([P, PASSES, 4 * P], U8, align_bytes=64)
            nc.vector.quantize_mx(
                out=codes01[:].rearrange("p g c -> p (g c)").bitcast(FP8X4),
                scales=planes01[:].rearrange("p g c -> p (g c)"),
                in_=xn_tiles[pair][0][:].rearrange("p g j i c -> p (g j i c)"),
            )
            operand_tiles[pair, 0] = (codes01, planes01)

        def quantise2(pair):
            codes2 = work.tile([P, PASSES, 2 * P], U32, align_bytes=64)
            planes2 = work.tile([P, PASSES, 2 * P], U8, align_bytes=64)
            nc.vector.quantize_mx(
                out=codes2[:].rearrange("p g c -> p (g c)").bitcast(FP8X4),
                scales=planes2[:].rearrange("p g c -> p (g c)"),
                in_=xn_tiles[pair][1][:].rearrange("p g i c -> p (g i c)"),
            )
            operand_tiles[pair, 2] = (codes2, planes2)

        def multiply(pair):
            if pair < PAIRS - 1:
                right01 = acc_psum.tile([P, 2 * 2 * P], F32, tag="right01")
                both2 = acc_psum.tile([P, 2, 2 * P], F32, tag="both2")
                left01 = acc_psum.tile([P, 2 * 2 * P], F32, tag="left01")
            else:
                right01 = words_psum.tile([P, 2 * 2 * P], F32, tag="xT")
                left01 = words_psum.tile([P, 2 * 2 * P], F32, tag="xT")
                both2 = words_psum.tile([P, 2, 2 * P], F32, tag="xT")
            products = ((RIGHT, 0, right01[:]), (RIGHT, 2, both2[:, 0, :]), (LEFT, 2, both2[:, 1, :]), (LEFT, 0, left01[:]))
            if pair == PAIRS - 1:
                products = (products[0], products[3], products[1], products[2])
            for side, j, acc in products:
                codes, planes = operand_tiles[pair, j]
                for g in range(PASSES):
                    nc.tensor.matmul_mx(
                        out=acc,
                        lhsT=w_codes[:, side + g, :].bitcast(FP8X4),
                        lhsT_scale=w_planes[:, side + g, :],
                        rhs=codes[:, g, :].bitcast(FP8X4),
                        rhs_scale=planes[:, g, :],
                        start=(g == 0),
                        stop=(g == PASSES - 1),
                    )
            product_tiles[pair] = (right01, both2, left01)

        def copy_right(pair):
            right01, both2, left01 = product_tiles[pair]
            right_sb = work.tile([P, COMPONENTS, 2 * P], F32)
            nc.scalar.copy(out=right_sb[:, 0:2, :].rearrange("p j c -> p (j c)"), in_=right01[:])
            nc.scalar.copy(out=right_sb[:, 2, :], in_=both2[:, 0, :])
            right_tiles[pair] = right_sb

        def combine(pair):
            right01, both2, left01 = product_tiles[pair]
            right_sb = right_tiles[pair]
            terms = work.tile([P, COMPONENTS, 2, P], F32)
            thirds = (terms[:, 2].rearrange("p i b -> p (i b)"), both2[:, 1, :], right_sb[:, 2, :])
            others = (terms[:, 0:2].rearrange("p j i b -> p (j i b)"), left01[:], right_sb[:, 0:2, :].rearrange("p j c -> p (j c)"))
            for product, left, right in (thirds, others) if pair < PAIRS - 1 else (others, thirds):
                nc.vector.tensor_tensor(out=product, in0=left, in1=right, op=ALU.mult)
            term_tiles[pair] = terms

        def add_up(pair):
            if pair < PAIRS - DRAIN_PAIRS:
                sums = acc_psum.tile([P, 2, HIDDEN], F32, tag="right01")
            else:
                sums = lengths_psum.tile([P, 2, HIDDEN], F32, tag="small")
            for i in range(2):
                sources = [rows_all[:, 2 * pair + i, :]] + [term_tiles[pair][:, j, i, :] for j in range(COMPONENTS)]
                for s in range(len(sources)):
                    nc.tensor.matmul(
                        out=sums[:, i, :],
                        lhsT=sources[s],
                        rhs=identity[:],
                        is_transpose=True,
                        start=(s == 0),
                        stop=(s == COMPONENTS),
                    )
            sum_tiles[pair] = sums

        def collect(pair):
            nc.vector.tensor_copy(out=rows_all[:, 2 * pair : 2 * pair + 2, :], in_=sum_tiles[pair][:])

        def collect_tanh(pair):
            nc.scalar.activation(out=rows_all[:, 2 * pair : 2 * pair + 2, :], in_=sum_tiles[pair][:], func=ACT.Tanh)

        def store(begin, end):
            nc.sync.dma_start(out=out_rows[:, begin:end, :], in_=rows_all[:, begin:end, :])

        def finish(begin, end):
            nc.scalar.activation(out=rows_all[:, begin:end, :], in_=rows_all[:, begin:end, :], func=ACT.Tanh)
            store(begin, end)

        def due(step, stage):
            pair, rest = divmod(step - stage, 2)
            return pair if rest == 0 and 0 <= pair < PAIRS else None

        for t in range(LOAD_AHEAD):
            load(t)
            if t == 0:
                load_invariants(0)
        late_squares(0)

        quad_by_step = {quad_step(quad): quad for quad in range(QUADS)}
        linear_by_step = {linear_step(quad): quad for quad in range(QUADS)}
        for step in range(TILES + LENGTHS_STEP):
            if step + LOAD_AHEAD < TILES:
                load(step + LOAD_AHEAD)
            if step + LOAD_AHEAD in quad_by_step:
                load_invariants(quad_by_step[step + LOAD_AHEAD])
            if step == 1:
                load_weight(nc, w_codes, w_planes, LINEAR, W_ii_words, W_ii_scales)
                load_weight(nc, w_codes, w_planes, LEFT, W_left_words, W_left_scales)
                load_weight(nc, w_codes, w_planes, RIGHT, W_right_words, W_right_scales)
                nc.sync.dma_start(out=bias_column[:], in_=b_ii.rearrange("(h o) -> h o", o=1))
            pair = due(step, COMBINE_STEP)
            if pair is not None:
                copy_right(pair)
                combine(pair)
            if 0 <= step - LENGTHS_STEP < TILES:
                inverse_lengths(step - LENGTHS_STEP)
            if 0 <= step - NORMALISE_STEP < TILES:
                for j in range(COMPONENTS):
                    transpose_words(step - NORMALISE_STEP, j)
                    normalise(step - NORMALISE_STEP, j)
            pair = due(step, ADD_UP_STEP)
            if pair is not None:
                add_up(pair)
            pair = due(step, QUANTISE_STEP)
            if pair is not None:
                quantise01(pair)
                quantise2(pair)
            if step + 1 < TILES:
                late_squares(step + 1)
            if step - 1 in quad_by_step:
                quantise_invariants(quad_by_step[step - 1])
            if step in linear_by_step:
                linear_product(linear_by_step[step])
            pair = due(step, MULTIPLY_STEP)
            if pair is not None:
                multiply(pair)
            if step < TILES:
                early_squares(step)
            pair = due(step, ADD_UP_STEP)
            if pair is not None:
                collect(pair)
            if 0 <= step - LENGTHS_STEP < TILES:
                factors(step - LENGTHS_STEP)
            if step in linear_by_step:
                linear_terms(linear_by_step[step])
            if step in quad_by_step:
                turn_invariants(quad_by_step[step])

        last_tile, last_pair = TILES - 1, PAIRS - 1
        stored = TILES - 2 * DRAIN_PAIRS
        copy_right(last_pair - 2)
        combine(last_pair - 2)
        for j in range(COMPONENTS):
            transpose_words(last_tile, j)
        normalise(last_tile, 0)
        normalise(last_tile, 1)
        quantise01(last_pair)
        normalise(last_tile, 2)
        add_up(last_pair - 3)
        multiply(last_pair - 1)
        collect_tanh(last_pair - 3)
        finish(0, stored // 2)
        copy_right(last_pair - 1)
        quantise2(last_pair)
        combine(last_pair - 1)
        add_up(last_pair - 2)
        multiply(last_pair)
        collect_tanh(last_pair - 2)
        finish(stored // 2, stored)
        add_up(last_pair - 1)
        copy_right(last_pair)
        collect_tanh(last_pair - 1)
        store(stored, TILES - 2)
        combine(last_pair)
        add_up(last_pair)
        collect_tanh(last_pair)
        store(TILES - 2, TILES)
